import numpy as np
import ml_dtypes


def mxq(x, axis, fmt="e4m3"):
    dtype, down = {"e4m3": (ml_dtypes.float8_e4m3fn, 7), "e5m2": (ml_dtypes.float8_e5m2, 14)}[fmt]
    v = np.moveaxis(np.asarray(x, np.float32).astype(ml_dtypes.bfloat16).astype(np.float64), axis, -1)
    blocks = v.reshape(v.shape[:-1] + (-1, 32))
    amax = np.abs(blocks).max(-1, keepdims=True)
    byte = np.maximum(np.where(amax > 0, np.frexp(amax)[1] - 1 + 127, 0) - down, 1)
    scale = np.exp2(byte - 127.0)
    codes = (blocks / scale).astype(np.float32).astype(dtype).astype(np.float64)
    return np.moveaxis((codes * scale).reshape(v.shape), -1, axis)


WIDE = False


def mx_kscale(k):
    if not WIDE:
        return np.ones(k)
    levels = np.array([10, -10, 5, -5, 0])
    a = np.random.permutation(np.resize(levels, k // 512 * 4)).reshape(k // 512, 4)
    idx = np.arange(k)
    return np.exp2(a[idx // 512, idx % 128 // 32])


BF16 = ml_dtypes.bfloat16


def bf(x):
    return np.asarray(x, np.float32).astype(BF16)


def f64(x):
    return np.asarray(x).astype(np.float64)


B, N, H, T1 = 2, 4096, 512, 3072


def sigmoid(x):
    return 1.0 / (1.0 + np.exp(-x))


def setup_inputs():
    s = mx_kscale(H)
    w = 1.0 / np.sqrt(H)
    return {"hidden_states": bf(np.random.standard_normal((B, N, H))),
            "acc": bf(np.random.standard_normal((B, N, H)) * s),
            "Wu_inter": bf(np.random.standard_normal((H, H)) * w / s),
            "bu_inter": bf(np.random.standard_normal(H) * 0.3),
            "Wt_inter": bf(np.random.standard_normal((H, H)) * w),
            "bt_inter": bf(np.random.standard_normal(H) * 0.3),
            "Wu_out": bf(np.random.standard_normal((H, H)) * w / s),
            "bu_out": bf(np.random.standard_normal(H) * 0.3),
            "Wt_out": bf(np.random.standard_normal((H, H)) * w),
            "bt_out": bf(np.random.standard_normal(H) * 0.3),
            "step_size": bf(0.5 + 0.5 * np.random.uniform(size=(1,)))}


def branch(h, hq, aq, Wu, bu, Wt, bt, step):
    dt = 2.0 * sigmoid((hq @ mxq(f64(Wt), 1, "e4m3").T) + f64(bt)) - 1.0
    return h + step * dt * ((aq @ mxq(f64(Wu), 1, "e4m3").T) + f64(bu))


def reference(hidden_states, acc, Wu_inter, bu_inter, Wt_inter, bt_inter, Wu_out, bu_out, Wt_out, bt_out, step_size):
    h = f64(hidden_states)
    hq = mxq(h, 2, "e4m3")
    aq = mxq(f64(acc), 2, "e4m3")
    step = f64(step_size)
    upd_inter = branch(h[:, :T1], hq[:, :T1], aq[:, :T1], Wu_inter, bu_inter, Wt_inter, bt_inter, step)
    upd_out = branch(h[:, T1:], hq[:, T1:], aq[:, T1:], Wu_out, bu_out, Wt_out, bt_out, step)
    return np.concatenate([upd_inter, upd_out], axis=1)

@@ -1,0 +1,247 @@
+from contextlib import ExitStack
+
+import concourse.bass as bass
+import concourse.mybir as mybir
+import concourse.tile as tile
+from concourse.masks import make_identity
+
+F32 = mybir.dt.float32
+BF16 = mybir.dt.bfloat16
+U32 = mybir.dt.uint32
+U8 = mybir.dt.uint8
+FP8X4 = mybir.dt.float8_e4m3fn_x4
+ACT = mybir.ActivationFunctionType
+ALU = mybir.AluOpType
+
+P = 128
+H = 512
+FLOPS = 2 * 2 * 8192 * 512 * 512
+
+SUPER = [(0, 0, 0), (0, 1024, 0), (0, 2048, 0), (1, 0, 0), (1, 1024, 0), (1, 2048, 0), (0, 3072, 1), (1, 3072, 1)]
+NG = 16
+GF = (3,)
+
+
+def tile_dynamicattentionnetwork_pb_t_kernel(
+    tc, hidden_states, acc, Wu_inter, bu_inter, Wt_inter, bt_inter, Wu_out, bu_out, Wt_out, bt_out, step_size, out
+):
+    nc = tc.nc
+    with ExitStack() as ctx:
+        ctx.enter_context(tc.manual_schedule())
+        const = ctx.enter_context(tc.tile_pool(name="const", bufs=1))
+        xin = ctx.enter_context(tc.tile_pool(name="xin", bufs=3))
+        wraw = ctx.enter_context(tc.tile_pool(name="wraw", bufs=2))
+        grp = ctx.enter_context(tc.tile_pool(name="grp", bufs=2))
+        cod = ctx.enter_context(tc.tile_pool(name="cod", bufs=2))
+        mid = ctx.enter_context(tc.tile_pool(name="mid", bufs=3))
+        res = ctx.enter_context(tc.tile_pool(name="res", bufs=3))
+        psum = ctx.enter_context(tc.psum_pool(name="psum", bufs=8))
+
+        def bank():
+            return psum.tile([P, 512], F32, name="bank", tag="bank")
+
+        warm = const.tile([P, 1], F32, name="warm", tag="warm")
+        nc.vector.memset(warm[:], 0.0)
+        nc.scalar.activation(out=warm[:], in_=warm[:], func=ACT.Tanh)
+        ident = const.tile([P, P], F32, name="ident", tag="ident")
+        make_identity(nc, ident[:])
+        brow = const.tile([P, P], BF16, name="brow", tag="brow")
+        nc.vector.memset(brow[:], 0.0)
+        for n, b in enumerate((bt_inter, bu_inter, bt_out, bu_out)):
+            nc.scalar.dma_start(out=brow[4 * n : 4 * n + 4, :], in_=b.rearrange("(a c) -> a c", c=P))
+        step_bf = const.tile([P, 1], BF16, name="step_bf", tag="step_bf")
+        nc.scalar.dma_start(out=step_bf[:], in_=step_size.partition_broadcast(P))
+        step = const.tile([P, 1], F32, name="step", tag="step")
+        brow32 = const.tile([P, P], F32, name="brow32", tag="brow32")
+        bias = const.tile([P, 16], F32, name="bias", tag="bias")
+        bhalf = const.tile([P, 16], F32, name="bhalf", tag="bhalf")
+
+        xs = {}
+
+        def load_super(s, parts):
+            b, n0 = SUPER[s][0], SUPER[s][1]
+            ht = xin.tile([P, 8 * H], BF16, name="h_sb", tag="h_sb")
+            at = xin.tile([P, 8 * H], BF16, name="a_sb", tag="a_sb")
+            xs[s] = (ht, at)
+            hv = hidden_states[b, n0 : n0 + 1024, :].rearrange("(p j) k -> p (j k)", j=8)
+            av = acc[b, n0 : n0 + 1024, :].rearrange("(p j) k -> p (j k)", j=8)
+            w = 8 * H // parts
+            todo = []
+            for c in range(parts):
+                todo.append((ht[:, c * w : (c + 1) * w], hv[:, c * w : (c + 1) * w]))
+                todo.append((at[:, c * w : (c + 1) * w], av[:, c * w : (c + 1) * w]))
+            return todo
+
+        def issue(todo):
+            for dst, src in todo:
+                nc.sync.dma_start(out=dst, in_=src)
+
+        wts = {}
+
+        def load_weight(key, w):
+            t = wraw.tile([P, 4 * H], BF16, name="w_sb", tag="w_sb")
+            nc.sync.dma_start(out=t[:].rearrange("p (j k) -> p j k", j=4), in_=w.rearrange("(j p) k -> p j k", p=P))
+            wts[key] = t
+
+        def t_in(words, half):
+            ps = bank()
+            pv = ps[:].rearrange("p (u r) -> p u r", u=2)
+            for jj in range(2):
+                for u in range(2):
+                    c0 = 256 * (2 * half + jj) + 128 * u
+                    nc.tensor.transpose(pv[:, u, 128 * jj : 128 * jj + 128], words[:, c0 : c0 + 128], ident[:])
+            return ps
+
+        def t_exit(eng, ps, g_tile, half):
+            dst = g_tile[:].bitcast(F32)[:, 512 * half : 512 * half + 512].rearrange("p (r u) -> p r u", u=2)
+            src = ps[:].rearrange("p (u r) -> p r u", u=2)
+            if eng == "s":
+                nc.scalar.copy(out=dst, in_=src)
+            else:
+                nc.vector.tensor_copy(out=dst, in_=src)
+
+        def quant(g_tile, pool, tag):
+            c = pool.tile([P, 512], U32, name="c_" + tag, tag="c_" + tag, align_bytes=64)
+            s = pool.tile([P, 512], U8, name="s_" + tag, tag="s_" + tag, align_bytes=64)
+            nc.vector.quantize_mx(out=c[:].bitcast(FP8X4), scales=s[:], in_=g_tile[:])
+            return (c, s)
+
+        def new_grouped(tag):
+            return grp.tile([P, 2048], BF16, name="g_" + tag, tag="g_" + tag, align_bytes=64)
+
+        def words_of(g, op):
+            return xs[g // 2][op][:].bitcast(F32)[:, 1024 * (g % 2) : 1024 * (g % 2) + 1024]
+
+        grouped = {}
+        codes = {}
+        wcodes = {}
+
+        first = load_super(0, 2)
+        load_weight("t0", Wt_inter)
+        issue(first[0:1])
+        load_weight("u0", Wu_inter)
+        issue(first[1:])
+        issue(load_super(1, 1))
+        issue(load_super(2, 1))
+
+        def prep_weight_t(key, engs):
+            g_t = new_grouped("w")
+            for half in range(2):
+                ps = t_in(wts[key][:].bitcast(F32), half)
+                t_exit(engs[half], ps, g_t, half)
+            return g_t
+
+        gw = prep_weight_t("t0", "sv")
+        grouped[(0, 0)] = new_grouped("h")
+        for half in range(2):
+            ps = t_in(words_of(0, 0), half)
+            t_exit("sv"[half], ps, grouped[(0, 0)], half)
+        wcodes["t0"] = quant(gw, const, "wt0")
+        gw = prep_weight_t("u0", "sv")
+        codes[(0, 0)] = quant(grouped[(0, 0)], cod, "h")
+        grouped[(0, 1)] = new_grouped("a")
+        for half in range(2):
+            ps = t_in(words_of(0, 1), half)
+            t_exit("sv"[half], ps, grouped[(0, 1)], half)
+        wcodes["u0"] = quant(gw, const, "wu0")
+        codes[(0, 1)] = quant(grouped[(0, 1)], cod, "a")
+        nc.vector.tensor_copy(out=brow32[:], in_=brow[:])
+        nc.vector.tensor_copy(out=step[:], in_=step_bf[:])
+        psb = bank()
+        nc.tensor.transpose(psb[:, 0:P], brow32[:], ident[:])
+        nc.vector.tensor_copy(out=bias[:], in_=psb[:, 0:16])
+        nc.scalar.mul(out=bhalf[:], in_=bias[:], mul=0.5)
+        for op in range(2):
+            grouped[(1, op)] = new_grouped("ha"[op])
+            for half in range(2):
+                ps = t_in(words_of(1, op), half)
+                t_exit("sv"[half], ps, grouped[(1, op)], half)
+        load_weight("t1", Wt_out)
+        load_weight("u1", Wu_out)
+
+        extra = {3: "t1", 5: "u1"}
+        pending_w = []
+
+        for i in range(NG):
+            s_i = i // 2
+            typ = SUPER[s_i][2]
+            j0 = 4 * (i % 2)
+            if i % 2 == 0 and 3 <= (i + 4) // 2 < 8:
+                issue(load_super((i + 4) // 2, 1))
+            if i + 1 < NG:
+                for op in range(2):
+                    codes[(i + 1, op)] = quant(grouped[(i + 1, op)], cod, "ha"[op])
+            for key, g_t in pending_w:
+                wcodes[key] = quant(g_t, const, "w" + key)
+            pending_w = []
+            hc, hs = codes[(i, 0)]
+            ac, asc = codes[(i, 1)]
+            tc_, ts_ = wcodes["t%d" % typ]
+            uc_, us_ = wcodes["u%d" % typ]
+            mts = []
+            for fb in range(4):
+                cols = slice(128 * fb, 128 * fb + 128)
+                ps_t = bank()
+                nc.tensor.matmul_mx(
+                    out=ps_t[:], lhsT=tc_[:, cols].bitcast(FP8X4), lhsT_scale=ts_[:, cols],
+                    rhs=hc[:].bitcast(FP8X4), rhs_scale=hs[:], start=True, stop=True,
+                )
+                ps_u = bank()
+                nc.tensor.matmul_mx(
+                    out=ps_u[:], lhsT=uc_[:, cols].bitcast(FP8X4), lhsT_scale=us_[:, cols],
+                    rhs=ac[:].bitcast(FP8X4), rhs_scale=asc[:], start=True, stop=True,
+                )
+                dt = mid.tile([P, 512], F32, name="dt", tag="dt")
+                bt_col = 8 * typ + fb
+                bu_col = 8 * typ + 4 + fb
+                nc.scalar.activation(
+                    out=dt[:], in_=ps_t[:], func=ACT.Tanh, bias=bhalf[:, bt_col : bt_col + 1], scale=0.5
+                )
+                mt = mid.tile([P, 512], F32, name="mt", tag="mt", bufs=6)
+                nc.vector.scalar_tensor_tensor(
+                    out=mt[:], in0=ps_u[:], scalar=bias[:, bu_col : bu_col + 1], in1=dt[:], op0=ALU.add, op1=ALU.mult
+                )
+                mts.append(mt)
+
+            o = res.tile([P, 4, H], F32, name="o", tag="o")
+            h3 = xs[s_i][0][:].rearrange("p (j k) -> p j k", j=8)
+
+            def t_out(fb):
+                ps = bank()
+                for jl in range(4):
+                    nc.tensor.transpose(ps[:, 128 * jl : 128 * jl + 128], mts[fb][:, 128 * jl : 128 * jl + 128], ident[:])
+                cols = slice(128 * fb, 128 * fb + 128)
+                p3 = ps[:].rearrange("p (j f) -> p j f", j=4)
+                if fb in GF:
+                    ms = mid.tile([P, 4, P], F32, name="ms", tag="ms", bufs=2)
+                    nc.scalar.activation(out=ms[:], in_=p3, func=ACT.Copy, scale=step[:, 0:1])
+                    nc.gpsimd.tensor_tensor(out=o[:, :, cols], in0=ms[:], in1=h3[:, j0 : j0 + 4, cols], op=ALU.add)
+                else:
+                    nc.vector.scalar_tensor_tensor(
+                        out=o[:, :, cols], in0=p3, scalar=step[:, 0:1], in1=h3[:, j0 : j0 + 4, cols],
+                        op0=ALU.mult, op1=ALU.add,
+                    )
+
+            def t_next(b):
+                g = i + 2
+                if g >= NG:
+                    return
+                op, half = b // 2, b % 2
+                if half == 0:
+                    grouped[(g, op)] = new_grouped("ha"[op])
+                ps = t_in(words_of(g, op), half)
+                t_exit("s", ps, grouped[(g, op)], half)
+
+            t_next(0)
+            t_next(1)
+            t_out(0)
+            t_next(2)
+            t_out(1)
+            t_next(3)
+            t_out(2)
+            t_out(3)
+            if i in extra:
+                pending_w.append((extra[i], prep_weight_t(extra[i], "sv")))
+            b, n0 = SUPER[s_i][0], SUPER[s_i][1]
+            ov = out[b, n0 : n0 + 1024, :].rearrange("(p j) f -> p j f", j=8)
+            nc.sync.dma_start(out=ov[:, j0 : j0 + 4, :], in_=o[:])

@@ -1,8 +1,6 @@
 from contextlib import ExitStack
 
-import concourse.bass as bass
 import concourse.mybir as mybir
-import concourse.tile as tile
 from concourse.masks import make_identity
 
 F32 = mybir.dt.float32
@@ -17,9 +15,10 @@ P = 128
 H = 512
 FLOPS = 2 * 2 * 8192 * 512 * 512
 
-SUPER = [(0, 0, 0), (0, 1024, 0), (0, 2048, 0), (1, 0, 0), (1, 1024, 0), (1, 2048, 0), (0, 3072, 1), (1, 3072, 1)]
-NG = 16
-GF = (3,)
+BLOCKS = [(0, 0, 0), (0, 1024, 0), (0, 2048, 0), (1, 0, 0), (1, 1024, 0), (1, 2048, 0), (0, 3072, 1), (1, 3072, 1)]
+GROUPS = 16
+AHEAD = 3
+LATE_WEIGHTS = {2: "t1", 4: "u1"}
 
 
 def tile_dynamicattentionnetwork_pb_t_kernel(
@@ -29,7 +28,7 @@ def tile_dynamicattentionnetwork_pb_t_kernel(
     with ExitStack() as ctx:
         ctx.enter_context(tc.manual_schedule())
         const = ctx.enter_context(tc.tile_pool(name="const", bufs=1))
-        xin = ctx.enter_context(tc.tile_pool(name="xin", bufs=3))
+        xin = ctx.enter_context(tc.tile_pool(name="xin", bufs=4))
         wraw = ctx.enter_context(tc.tile_pool(name="wraw", bufs=2))
         grp = ctx.enter_context(tc.tile_pool(name="grp", bufs=2))
         cod = ctx.enter_context(tc.tile_pool(name="cod", bufs=2))
@@ -58,23 +57,16 @@ def tile_dynamicattentionnetwork_pb_t_kernel(
 
         xs = {}
 
-        def load_super(s, parts):
-            b, n0 = SUPER[s][0], SUPER[s][1]
+        def block_tiles(s):
             ht = xin.tile([P, 8 * H], BF16, name="h_sb", tag="h_sb")
-            at = xin.tile([P, 8 * H], BF16, name="a_sb", tag="a_sb")
+            at = xin.tile([P, 8 * H], BF16, name="a_sb", tag="a_sb", bufs=3)
             xs[s] = (ht, at)
-            hv = hidden_states[b, n0 : n0 + 1024, :].rearrange("(p j) k -> p (j k)", j=8)
-            av = acc[b, n0 : n0 + 1024, :].rearrange("(p j) k -> p (j k)", j=8)
-            w = 8 * H // parts
-            todo = []
-            for c in range(parts):
-                todo.append((ht[:, c * w : (c + 1) * w], hv[:, c * w : (c + 1) * w]))
-                todo.append((at[:, c * w : (c + 1) * w], av[:, c * w : (c + 1) * w]))
-            return todo
 
-        def issue(todo):
-            for dst, src in todo:
-                nc.sync.dma_start(out=dst, in_=src)
+        def load_block(s, op, part, parts):
+            b, n0 = BLOCKS[s][0], BLOCKS[s][1]
+            src = (hidden_states, acc)[op][b, n0 : n0 + 1024, :].rearrange("(p j) k -> p (j k)", j=8)
+            w = 8 * H // parts
+            nc.sync.dma_start(out=xs[s][op][:, part * w : (part + 1) * w], in_=src[:, part * w : (part + 1) * w])
 
         wts = {}
 
@@ -83,31 +75,28 @@ def tile_dynamicattentionnetwork_pb_t_kernel(
             nc.sync.dma_start(out=t[:].rearrange("p (j k) -> p j k", j=4), in_=w.rearrange("(j p) k -> p j k", p=P))
             wts[key] = t
 
-        def t_in(words, half):
-            ps = bank()
-            pv = ps[:].rearrange("p (u r) -> p u r", u=2)
-            for jj in range(2):
-                for u in range(2):
-                    c0 = 256 * (2 * half + jj) + 128 * u
-                    nc.tensor.transpose(pv[:, u, 128 * jj : 128 * jj + 128], words[:, c0 : c0 + 128], ident[:])
-            return ps
+        def transpose_in(words, tag, engines):
+            g_tile = grp.tile([P, 2048], BF16, name="g_" + tag, tag="g_" + tag, align_bytes=64)
+            for half in range(2):
+                ps = bank()
+                pv = ps[:].rearrange("p (u r) -> p u r", u=2)
+                for jj in range(2):
+                    for u in range(2):
+                        c0 = 256 * (2 * half + jj) + 128 * u
+                        nc.tensor.transpose(pv[:, u, 128 * jj : 128 * jj + 128], words[:, c0 : c0 + 128], ident[:])
+                dst = g_tile[:].bitcast(F32)[:, 512 * half : 512 * half + 512].rearrange("p (r u) -> p r u", u=2)
+                src = ps[:].rearrange("p (u r) -> p r u", u=2)
+                if engines[half] == "s":
+                    nc.scalar.copy(out=dst, in_=src)
+                else:
+                    nc.vector.tensor_copy(out=dst, in_=src)
+            return g_tile
 
-        def t_exit(eng, ps, g_tile, half):
-            dst = g_tile[:].bitcast(F32)[:, 512 * half : 512 * half + 512].rearrange("p (r u) -> p r u", u=2)
-            src = ps[:].rearrange("p (u r) -> p r u", u=2)
-            if eng == "s":
-                nc.scalar.copy(out=dst, in_=src)
-            else:
-                nc.vector.tensor_copy(out=dst, in_=src)
-
-        def quant(g_tile, pool, tag):
+        def quantise(g_tile, pool, tag):
             c = pool.tile([P, 512], U32, name="c_" + tag, tag="c_" + tag, align_bytes=64)
             s = pool.tile([P, 512], U8, name="s_" + tag, tag="s_" + tag, align_bytes=64)
             nc.vector.quantize_mx(out=c[:].bitcast(FP8X4), scales=s[:], in_=g_tile[:])
             return (c, s)
-
-        def new_grouped(tag):
-            return grp.tile([P, 2048], BF16, name="g_" + tag, tag="g_" + tag, align_bytes=64)
 
         def words_of(g, op):
             return xs[g // 2][op][:].bitcast(F32)[:, 1024 * (g % 2) : 1024 * (g % 2) + 1024]
@@ -116,80 +105,77 @@ def tile_dynamicattentionnetwork_pb_t_kernel(
         codes = {}
         wcodes = {}
 
-        first = load_super(0, 2)
+        def group_in(g, engines):
+            for op in range(2):
+                grouped[(g, op)] = transpose_in(words_of(g, op), "ha"[op], engines)
+
+        def group_quantise(g):
+            for op in range(2):
+                codes[(g, op)] = quantise(grouped[(g, op)], cod, "ha"[op])
+
+        for s in range(3):
+            block_tiles(s)
         load_weight("t0", Wt_inter)
-        issue(first[0:1])
+        load_block(0, 0, 0, 2)
         load_weight("u0", Wu_inter)
-        issue(first[1:])
-        issue(load_super(1, 1))
-        issue(load_super(2, 1))
+        load_block(0, 1, 0, 2)
+        load_block(0, 0, 1, 2)
+        load_block(0, 1, 1, 2)
+        for part in range(2):
+            load_block(1, 0, part, 2)
+            load_block(1, 1, part, 2)
+        load_block(2, 0, 0, 1)
+        load_block(2, 1, 0, 1)
 
-        def prep_weight_t(key, engs):
-            g_t = new_grouped("w")
-            for half in range(2):
-                ps = t_in(wts[key][:].bitcast(F32), half)
-                t_exit(engs[half], ps, g_t, half)
-            return g_t
-
-        gw = prep_weight_t("t0", "sv")
-        grouped[(0, 0)] = new_grouped("h")
-        for half in range(2):
-            ps = t_in(words_of(0, 0), half)
-            t_exit("sv"[half], ps, grouped[(0, 0)], half)
-        wcodes["t0"] = quant(gw, const, "wt0")
-        gw = prep_weight_t("u0", "sv")
-        codes[(0, 0)] = quant(grouped[(0, 0)], cod, "h")
-        grouped[(0, 1)] = new_grouped("a")
-        for half in range(2):
-            ps = t_in(words_of(0, 1), half)
-            t_exit("sv"[half], ps, grouped[(0, 1)], half)
-        wcodes["u0"] = quant(gw, const, "wu0")
-        codes[(0, 1)] = quant(grouped[(0, 1)], cod, "a")
+        gw = transpose_in(wts["t0"][:].bitcast(F32), "w", "sv")
+        grouped[(0, 0)] = transpose_in(words_of(0, 0), "h", "sv")
+        wcodes["t0"] = quantise(gw, const, "wt0")
+        gw = transpose_in(wts["u0"][:].bitcast(F32), "w", "sv")
+        codes[(0, 0)] = quantise(grouped[(0, 0)], cod, "h")
+        grouped[(0, 1)] = transpose_in(words_of(0, 1), "a", "sv")
+        wcodes["u0"] = quantise(gw, const, "wu0")
+        codes[(0, 1)] = quantise(grouped[(0, 1)], cod, "a")
+        load_weight("t1", Wt_out)
+        load_weight("u1", Wu_out)
         nc.vector.tensor_copy(out=brow32[:], in_=brow[:])
         nc.vector.tensor_copy(out=step[:], in_=step_bf[:])
         psb = bank()
         nc.tensor.transpose(psb[:, 0:P], brow32[:], ident[:])
         nc.vector.tensor_copy(out=bias[:], in_=psb[:, 0:16])
         nc.scalar.mul(out=bhalf[:], in_=bias[:], mul=0.5)
-        for op in range(2):
-            grouped[(1, op)] = new_grouped("ha"[op])
-            for half in range(2):
-                ps = t_in(words_of(1, op), half)
-                t_exit("sv"[half], ps, grouped[(1, op)], half)
-        load_weight("t1", Wt_out)
-        load_weight("u1", Wu_out)
+        group_in(1, "sv")
+        group_quantise(1)
+        block_tiles(3)
+        load_block(3, 0, 0, 1)
+        load_block(3, 1, 0, 1)
+        group_in(2, "sv")
 
-        extra = {3: "t1", 5: "u1"}
-        pending_w = []
+        waiting_weights = []
 
-        for i in range(NG):
+        for i in range(GROUPS):
             s_i = i // 2
-            typ = SUPER[s_i][2]
+            b, n0, typ = BLOCKS[s_i]
             j0 = 4 * (i % 2)
-            if i % 2 == 0 and 3 <= (i + 4) // 2 < 8:
-                issue(load_super((i + 4) // 2, 1))
-            if i + 1 < NG:
-                for op in range(2):
-                    codes[(i + 1, op)] = quant(grouped[(i + 1, op)], cod, "ha"[op])
-            for key, g_t in pending_w:
-                wcodes[key] = quant(g_t, const, "w" + key)
-            pending_w = []
+            if i % 2 == 0 and 4 <= (i + 6) // 2 < 8:
+                block_tiles((i + 6) // 2)
+                load_block((i + 6) // 2, 0, 0, 1)
+                load_block((i + 6) // 2, 1, 0, 1)
             hc, hs = codes[(i, 0)]
             ac, asc = codes[(i, 1)]
-            tc_, ts_ = wcodes["t%d" % typ]
-            uc_, us_ = wcodes["u%d" % typ]
+            wtc, wtsc = wcodes["t%d" % typ]
+            wuc, wus = wcodes["u%d" % typ]
             mts = []
             for fb in range(4):
                 cols = slice(128 * fb, 128 * fb + 128)
-                ps_t = bank()
-                nc.tensor.matmul_mx(
-                    out=ps_t[:], lhsT=tc_[:, cols].bitcast(FP8X4), lhsT_scale=ts_[:, cols],
-                    rhs=hc[:].bitcast(FP8X4), rhs_scale=hs[:], start=True, stop=True,
-                )
                 ps_u = bank()
                 nc.tensor.matmul_mx(
-                    out=ps_u[:], lhsT=uc_[:, cols].bitcast(FP8X4), lhsT_scale=us_[:, cols],
+                    out=ps_u[:], lhsT=wuc[:, cols].bitcast(FP8X4), lhsT_scale=wus[:, cols],
                     rhs=ac[:].bitcast(FP8X4), rhs_scale=asc[:], start=True, stop=True,
+                )
+                ps_t = bank()
+                nc.tensor.matmul_mx(
+                    out=ps_t[:], lhsT=wtc[:, cols].bitcast(FP8X4), lhsT_scale=wtsc[:, cols],
+                    rhs=hc[:].bitcast(FP8X4), rhs_scale=hs[:], start=True, stop=True,
                 )
                 dt = mid.tile([P, 512], F32, name="dt", tag="dt")
                 bt_col = 8 * typ + fb
@@ -203,16 +189,28 @@ def tile_dynamicattentionnetwork_pb_t_kernel(
                 )
                 mts.append(mt)
 
+            if i + AHEAD - 1 < GROUPS:
+                group_quantise(i + AHEAD - 1)
+            for key, g_t in waiting_weights:
+                wcodes[key] = quantise(g_t, const, "w" + key)
+            waiting_weights = []
+
+            if i + AHEAD < GROUPS:
+                group_in(i + AHEAD, "ss")
+            if i in LATE_WEIGHTS:
+                key = LATE_WEIGHTS[i]
+                waiting_weights.append((key, transpose_in(wts[key][:].bitcast(F32), "w", "sv")))
+
             o = res.tile([P, 4, H], F32, name="o", tag="o")
             h3 = xs[s_i][0][:].rearrange("p (j k) -> p j k", j=8)
-
-            def t_out(fb):
+            ov = out[b, n0 : n0 + 1024, :].rearrange("(p j) f -> p j f", j=8)
+            for fb in range(4):
+                cols = slice(128 * fb, 128 * fb + 128)
                 ps = bank()
                 for jl in range(4):
                     nc.tensor.transpose(ps[:, 128 * jl : 128 * jl + 128], mts[fb][:, 128 * jl : 128 * jl + 128], ident[:])
-                cols = slice(128 * fb, 128 * fb + 128)
                 p3 = ps[:].rearrange("p (j f) -> p j f", j=4)
-                if fb in GF:
+                if fb == 3:
                     ms = mid.tile([P, 4, P], F32, name="ms", tag="ms", bufs=2)
                     nc.scalar.activation(out=ms[:], in_=p3, func=ACT.Copy, scale=step[:, 0:1])
                     nc.gpsimd.tensor_tensor(out=o[:, :, cols], in0=ms[:], in1=h3[:, j0 : j0 + 4, cols], op=ALU.add)
@@ -221,27 +219,7 @@ def tile_dynamicattentionnetwork_pb_t_kernel(
                         out=o[:, :, cols], in0=p3, scalar=step[:, 0:1], in1=h3[:, j0 : j0 + 4, cols],
                         op0=ALU.mult, op1=ALU.add,
                     )
-
-            def t_next(b):
-                g = i + 2
-                if g >= NG:
-                    return
-                op, half = b // 2, b % 2
-                if half == 0:
-                    grouped[(g, op)] = new_grouped("ha"[op])
-                ps = t_in(words_of(g, op), half)
-                t_exit("s", ps, grouped[(g, op)], half)
-
-            t_next(0)
-            t_next(1)
-            t_out(0)
-            t_next(2)
-            t_out(1)
-            t_next(3)
-            t_out(2)
-            t_out(3)
-            if i in extra:
-                pending_w.append((extra[i], prep_weight_t(extra[i], "sv")))
-            b, n0 = SUPER[s_i][0], SUPER[s_i][1]
-            ov = out[b, n0 : n0 + 1024, :].rearrange("(p j) f -> p j f", j=8)
-            nc.sync.dma_start(out=ov[:, j0 : j0 + 4, :], in_=o[:])
+                if i == GROUPS - 1:
+                    nc.sync.dma_start(out=ov[:, j0 : j0 + 4, cols], in_=o[:, :, cols])
+            if i < GROUPS - 1:
+                nc.sync.dma_start(out=ov[:, j0 : j0 + 4, :], in_=o[:])

@@ -17,8 +17,9 @@ FLOPS = 2 * 2 * 8192 * 512 * 512
 
 BLOCKS = [(0, 0, 0), (0, 1024, 0), (0, 2048, 0), (1, 0, 0), (1, 1024, 0), (1, 2048, 0), (0, 3072, 1), (1, 3072, 1)]
 GROUPS = 16
-AHEAD = 3
-LATE_WEIGHTS = {2: "t1", 4: "u1"}
+HALVES = 2 * GROUPS
+AHEAD = 2
+LATE_WEIGHTS = {6: "t1", 10: "u1"}
 
 
 def tile_dynamicattentionnetwork_pb_t_kernel(
@@ -121,11 +122,9 @@ def tile_dynamicattentionnetwork_pb_t_kernel(
         load_block(0, 1, 0, 2)
         load_block(0, 0, 1, 2)
         load_block(0, 1, 1, 2)
-        for part in range(2):
-            load_block(1, 0, part, 2)
-            load_block(1, 1, part, 2)
-        load_block(2, 0, 0, 1)
-        load_block(2, 1, 0, 1)
+        for s in (1, 2):
+            load_block(s, 0, 0, 1)
+            load_block(s, 1, 0, 1)
 
         gw = transpose_in(wts["t0"][:].bitcast(F32), "w", "sv")
         grouped[(0, 0)] = transpose_in(words_of(0, 0), "h", "sv")
@@ -145,72 +144,77 @@ def tile_dynamicattentionnetwork_pb_t_kernel(
         nc.scalar.mul(out=bhalf[:], in_=bias[:], mul=0.5)
         group_in(1, "sv")
         group_quantise(1)
-        block_tiles(3)
-        load_block(3, 0, 0, 1)
-        load_block(3, 1, 0, 1)
-        group_in(2, "sv")
 
-        waiting_weights = []
+        to_quantise = []
+        products = {}
+        results = {}
 
-        for i in range(GROUPS):
-            s_i = i // 2
-            b, n0, typ = BLOCKS[s_i]
+        for n in range(HALVES + 1):
+            i, hh = n // 2, n % 2
+            if n < HALVES:
+                typ = BLOCKS[i // 2][2]
+                if n % 4 == 0 and 3 <= (i + 4) // 2 < 8:
+                    block_tiles((i + 4) // 2)
+                    load_block((i + 4) // 2, 0, 0, 1)
+                    load_block((i + 4) // 2, 1, 0, 1)
+                hc, hs = codes[(i, 0)]
+                ac, asc = codes[(i, 1)]
+                wtc, wtsc = wcodes["t%d" % typ]
+                wuc, wus = wcodes["u%d" % typ]
+                for fb in (2 * hh, 2 * hh + 1):
+                    cols = slice(128 * fb, 128 * fb + 128)
+                    ps_u = bank()
+                    nc.tensor.matmul_mx(
+                        out=ps_u[:], lhsT=wuc[:, cols].bitcast(FP8X4), lhsT_scale=wus[:, cols],
+                        rhs=ac[:].bitcast(FP8X4), rhs_scale=asc[:], start=True, stop=True,
+                    )
+                    ps_t = bank()
+                    nc.tensor.matmul_mx(
+                        out=ps_t[:], lhsT=wtc[:, cols].bitcast(FP8X4), lhsT_scale=wtsc[:, cols],
+                        rhs=hc[:].bitcast(FP8X4), rhs_scale=hs[:], start=True, stop=True,
+                    )
+                    dt = mid.tile([P, 512], F32, name="dt", tag="dt")
+                    bt_col = 8 * typ + fb
+                    bu_col = 8 * typ + 4 + fb
+                    nc.scalar.activation(
+                        out=dt[:], in_=ps_t[:], func=ACT.Tanh, bias=bhalf[:, bt_col : bt_col + 1], scale=0.5
+                    )
+                    mt = mid.tile([P, 512], F32, name="mt", tag="mt", bufs=6)
+                    nc.vector.scalar_tensor_tensor(
+                        out=mt[:], in0=ps_u[:], scalar=bias[:, bu_col : bu_col + 1], in1=dt[:],
+                        op0=ALU.add, op1=ALU.mult,
+                    )
+                    products[(i, fb)] = mt
+
+                for where, key, g_t, pool, tag in to_quantise:
+                    where[key] = quantise(g_t, pool, tag)
+                to_quantise = []
+
+                g = i + AHEAD
+                if g < GROUPS:
+                    g_t = transpose_in(words_of(g, hh), "ha"[hh], "ss")
+                    to_quantise.append((codes, (g, hh), g_t, cod, "ha"[hh]))
+                if n in LATE_WEIGHTS:
+                    key = LATE_WEIGHTS[n]
+                    g_t = transpose_in(wts[key][:].bitcast(F32), "w", "sv")
+                    to_quantise.append((wcodes, key, g_t, const, "w" + key))
+
+            i, hh = max(n - 1, 0) // 2, max(n - 1, 0) % 2
+            b, n0 = BLOCKS[i // 2][0], BLOCKS[i // 2][1]
             j0 = 4 * (i % 2)
-            if i % 2 == 0 and 4 <= (i + 6) // 2 < 8:
-                block_tiles((i + 6) // 2)
-                load_block((i + 6) // 2, 0, 0, 1)
-                load_block((i + 6) // 2, 1, 0, 1)
-            hc, hs = codes[(i, 0)]
-            ac, asc = codes[(i, 1)]
-            wtc, wtsc = wcodes["t%d" % typ]
-            wuc, wus = wcodes["u%d" % typ]
-            mts = []
-            for fb in range(4):
-                cols = slice(128 * fb, 128 * fb + 128)
-                ps_u = bank()
-                nc.tensor.matmul_mx(
-                    out=ps_u[:], lhsT=wuc[:, cols].bitcast(FP8X4), lhsT_scale=wus[:, cols],
-                    rhs=ac[:].bitcast(FP8X4), rhs_scale=asc[:], start=True, stop=True,
-                )
-                ps_t = bank()
-                nc.tensor.matmul_mx(
-                    out=ps_t[:], lhsT=wtc[:, cols].bitcast(FP8X4), lhsT_scale=wtsc[:, cols],
-                    rhs=hc[:].bitcast(FP8X4), rhs_scale=hs[:], start=True, stop=True,
-                )
-                dt = mid.tile([P, 512], F32, name="dt", tag="dt")
-                bt_col = 8 * typ + fb
-                bu_col = 8 * typ + 4 + fb
-                nc.scalar.activation(
-                    out=dt[:], in_=ps_t[:], func=ACT.Tanh, bias=bhalf[:, bt_col : bt_col + 1], scale=0.5
-                )
-                mt = mid.tile([P, 512], F32, name="mt", tag="mt", bufs=6)
-                nc.vector.scalar_tensor_tensor(
-                    out=mt[:], in0=ps_u[:], scalar=bias[:, bu_col : bu_col + 1], in1=dt[:], op0=ALU.add, op1=ALU.mult
-                )
-                mts.append(mt)
-
-            if i + AHEAD - 1 < GROUPS:
-                group_quantise(i + AHEAD - 1)
-            for key, g_t in waiting_weights:
-                wcodes[key] = quantise(g_t, const, "w" + key)
-            waiting_weights = []
-
-            if i + AHEAD < GROUPS:
-                group_in(i + AHEAD, "ss")
-            if i in LATE_WEIGHTS:
-                key = LATE_WEIGHTS[i]
-                waiting_weights.append((key, transpose_in(wts[key][:].bitcast(F32), "w", "sv")))
-
-            o = res.tile([P, 4, H], F32, name="o", tag="o")
-            h3 = xs[s_i][0][:].rearrange("p (j k) -> p j k", j=8)
+            if hh == 0 and n > 0:
+                results[i] = res.tile([P, 4, H], F32, name="o", tag="o")
+            o = results.get(i)
+            h3 = xs[i // 2][0][:].rearrange("p (j k) -> p j k", j=8)
             ov = out[b, n0 : n0 + 1024, :].rearrange("(p j) f -> p j f", j=8)
-            for fb in range(4):
+            for fb in (2 * hh, 2 * hh + 1) if n > 0 else ():
                 cols = slice(128 * fb, 128 * fb + 128)
+                mt = products[(i, fb)]
                 ps = bank()
                 for jl in range(4):
-                    nc.tensor.transpose(ps[:, 128 * jl : 128 * jl + 128], mts[fb][:, 128 * jl : 128 * jl + 128], ident[:])
+                    nc.tensor.transpose(ps[:, 128 * jl : 128 * jl + 128], mt[:, 128 * jl : 128 * jl + 128], ident[:])
                 p3 = ps[:].rearrange("p (j f) -> p j f", j=4)
-                if fb == 3:
+                if fb == 0:
                     ms = mid.tile([P, 4, P], F32, name="ms", tag="ms", bufs=2)
                     nc.scalar.activation(out=ms[:], in_=p3, func=ACT.Copy, scale=step[:, 0:1])
                     nc.gpsimd.tensor_tensor(out=o[:, :, cols], in0=ms[:], in1=h3[:, j0 : j0 + 4, cols], op=ALU.add)
@@ -219,7 +223,8 @@ def tile_dynamicattentionnetwork_pb_t_kernel(
                         out=o[:, :, cols], in0=p3, scalar=step[:, 0:1], in1=h3[:, j0 : j0 + 4, cols],
                         op0=ALU.mult, op1=ALU.add,
                     )
-                if i == GROUPS - 1:
-                    nc.sync.dma_start(out=ov[:, j0 : j0 + 4, cols], in_=o[:, :, cols])
-            if i < GROUPS - 1:
+            if n > 0 and i == GROUPS - 1:
+                pair = slice(256 * hh, 256 * hh + 256)
+                nc.sync.dma_start(out=ov[:, j0 : j0 + 4, pair], in_=o[:, :, pair])
+            elif n > 0 and hh == 1:
                 nc.sync.dma_start(out=ov[:, j0 : j0 + 4, :], in_=o[:])

@@ -1,6 +1,8 @@
 from contextlib import ExitStack
 
+import concourse.bass as bass
 import concourse.mybir as mybir
+import concourse.tile as tile
 from concourse.masks import make_identity
 
 F32 = mybir.dt.float32
@@ -15,11 +17,9 @@ P = 128
 H = 512
 FLOPS = 2 * 2 * 8192 * 512 * 512
 
-BLOCKS = [(0, 0, 0), (0, 1024, 0), (0, 2048, 0), (1, 0, 0), (1, 1024, 0), (1, 2048, 0), (0, 3072, 1), (1, 3072, 1)]
-GROUPS = 16
-HALVES = 2 * GROUPS
-AHEAD = 2
-LATE_WEIGHTS = {6: "t1", 10: "u1"}
+SUPER = [(0, 0, 0), (0, 1024, 0), (0, 2048, 0), (1, 0, 0), (1, 1024, 0), (1, 2048, 0), (0, 3072, 1), (1, 3072, 1)]
+NG = 16
+GF = (3,)
 
 
 def tile_dynamicattentionnetwork_pb_t_kernel(
@@ -29,16 +29,17 @@ def tile_dynamicattentionnetwork_pb_t_kernel(
     with ExitStack() as ctx:
         ctx.enter_context(tc.manual_schedule())
         const = ctx.enter_context(tc.tile_pool(name="const", bufs=1))
-        xin = ctx.enter_context(tc.tile_pool(name="xin", bufs=4))
+        xin = ctx.enter_context(tc.tile_pool(name="xin", bufs=3))
         wraw = ctx.enter_context(tc.tile_pool(name="wraw", bufs=2))
         grp = ctx.enter_context(tc.tile_pool(name="grp", bufs=2))
         cod = ctx.enter_context(tc.tile_pool(name="cod", bufs=2))
         mid = ctx.enter_context(tc.tile_pool(name="mid", bufs=3))
         res = ctx.enter_context(tc.tile_pool(name="res", bufs=3))
-        psum = ctx.enter_context(tc.psum_pool(name="psum", bufs=8))
+        psum = ctx.enter_context(tc.psum_pool(name="psum", bufs=4))
 
-        def bank():
-            return psum.tile([P, 512], F32, name="bank", tag="bank")
+        def bank_pair():
+            t = psum.tile([P, 1024], F32, name="pair", tag="pair")
+            return (t[:, 0:512], t[:, 512:1024])
 
         warm = const.tile([P, 1], F32, name="warm", tag="warm")
         nc.vector.memset(warm[:], 0.0)
@@ -58,16 +59,23 @@ def tile_dynamicattentionnetwork_pb_t_kernel(
 
         xs = {}
 
-        def block_tiles(s):
+        def load_super(s, parts):
+            b, n0 = SUPER[s][0], SUPER[s][1]
             ht = xin.tile([P, 8 * H], BF16, name="h_sb", tag="h_sb")
-            at = xin.tile([P, 8 * H], BF16, name="a_sb", tag="a_sb", bufs=3)
+            at = xin.tile([P, 8 * H], BF16, name="a_sb", tag="a_sb")
             xs[s] = (ht, at)
-
-        def load_block(s, op, part, parts):
-            b, n0 = BLOCKS[s][0], BLOCKS[s][1]
-            src = (hidden_states, acc)[op][b, n0 : n0 + 1024, :].rearrange("(p j) k -> p (j k)", j=8)
+            hv = hidden_states[b, n0 : n0 + 1024, :].rearrange("(p j) k -> p (j k)", j=8)
+            av = acc[b, n0 : n0 + 1024, :].rearrange("(p j) k -> p (j k)", j=8)
             w = 8 * H // parts
-            nc.sync.dma_start(out=xs[s][op][:, part * w : (part + 1) * w], in_=src[:, part * w : (part + 1) * w])
+            todo = []
+            for c in range(parts):
+                todo.append((ht[:, c * w : (c + 1) * w], hv[:, c * w : (c + 1) * w]))
+                todo.append((at[:, c * w : (c + 1) * w], av[:, c * w : (c + 1) * w]))
+            return todo
+
+        def issue(todo):
+            for dst, src in todo:
+                nc.sync.dma_start(out=dst, in_=src)
 
         wts = {}
 
@@ -76,28 +84,29 @@ def tile_dynamicattentionnetwork_pb_t_kernel(
             nc.sync.dma_start(out=t[:].rearrange("p (j k) -> p j k", j=4), in_=w.rearrange("(j p) k -> p j k", p=P))
             wts[key] = t
 
-        def transpose_in(words, tag, engines):
-            g_tile = grp.tile([P, 2048], BF16, name="g_" + tag, tag="g_" + tag, align_bytes=64)
-            for half in range(2):
-                ps = bank()
-                pv = ps[:].rearrange("p (u r) -> p u r", u=2)
-                for jj in range(2):
-                    for u in range(2):
-                        c0 = 256 * (2 * half + jj) + 128 * u
-                        nc.tensor.transpose(pv[:, u, 128 * jj : 128 * jj + 128], words[:, c0 : c0 + 128], ident[:])
-                dst = g_tile[:].bitcast(F32)[:, 512 * half : 512 * half + 512].rearrange("p (r u) -> p r u", u=2)
-                src = ps[:].rearrange("p (u r) -> p r u", u=2)
-                if engines[half] == "s":
-                    nc.scalar.copy(out=dst, in_=src)
-                else:
-                    nc.vector.tensor_copy(out=dst, in_=src)
-            return g_tile
+        def t_in(ps, words, half):
+            pv = ps.rearrange("p (u r) -> p u r", u=2)
+            for jj in range(2):
+                for u in range(2):
+                    c0 = 256 * (2 * half + jj) + 128 * u
+                    nc.tensor.transpose(pv[:, u, 128 * jj : 128 * jj + 128], words[:, c0 : c0 + 128], ident[:])
 
-        def quantise(g_tile, pool, tag):
+        def t_exit(eng, ps, g_tile, half):
+            dst = g_tile[:].bitcast(F32)[:, 512 * half : 512 * half + 512].rearrange("p (r u) -> p r u", u=2)
+            src = ps.rearrange("p (u r) -> p r u", u=2)
+            if eng == "s":
+                nc.scalar.copy(out=dst, in_=src)
+            else:
+                nc.vector.tensor_copy(out=dst, in_=src)
+
+        def quant(g_tile, pool, tag):
             c = pool.tile([P, 512], U32, name="c_" + tag, tag="c_" + tag, align_bytes=64)
             s = pool.tile([P, 512], U8, name="s_" + tag, tag="s_" + tag, align_bytes=64)
             nc.vector.quantize_mx(out=c[:].bitcast(FP8X4), scales=s[:], in_=g_tile[:])
             return (c, s)
+
+        def new_grouped(tag):
+            return grp.tile([P, 2048], BF16, name="g_" + tag, tag="g_" + tag, align_bytes=64)
 
         def words_of(g, op):
             return xs[g // 2][op][:].bitcast(F32)[:, 1024 * (g % 2) : 1024 * (g % 2) + 1024]
@@ -106,125 +115,121 @@ def tile_dynamicattentionnetwork_pb_t_kernel(
         codes = {}
         wcodes = {}
 
-        def group_in(g, engines):
-            for op in range(2):
-                grouped[(g, op)] = transpose_in(words_of(g, op), "ha"[op], engines)
-
-        def group_quantise(g):
-            for op in range(2):
-                codes[(g, op)] = quantise(grouped[(g, op)], cod, "ha"[op])
-
-        for s in range(3):
-            block_tiles(s)
+        first = load_super(0, 2)
         load_weight("t0", Wt_inter)
-        load_block(0, 0, 0, 2)
+        issue(first[0:1])
         load_weight("u0", Wu_inter)
-        load_block(0, 1, 0, 2)
-        load_block(0, 0, 1, 2)
-        load_block(0, 1, 1, 2)
-        for s in (1, 2):
-            load_block(s, 0, 0, 1)
-            load_block(s, 1, 0, 1)
+        issue(first[1:])
+        issue(load_super(1, 1))
+        issue(load_super(2, 1))
 
-        gw = transpose_in(wts["t0"][:].bitcast(F32), "w", "sv")
-        grouped[(0, 0)] = transpose_in(words_of(0, 0), "h", "sv")
-        wcodes["t0"] = quantise(gw, const, "wt0")
-        gw = transpose_in(wts["u0"][:].bitcast(F32), "w", "sv")
-        codes[(0, 0)] = quantise(grouped[(0, 0)], cod, "h")
-        grouped[(0, 1)] = transpose_in(words_of(0, 1), "a", "sv")
-        wcodes["u0"] = quantise(gw, const, "wu0")
-        codes[(0, 1)] = quantise(grouped[(0, 1)], cod, "a")
-        load_weight("t1", Wt_out)
-        load_weight("u1", Wu_out)
+        def prep(words, tag, engs):
+            g_t = new_grouped(tag)
+            pair = bank_pair()
+            for half in range(2):
+                t_in(pair[half], words, half)
+            for half in range(2):
+                t_exit(engs[half], pair[half], g_t, half)
+            return g_t
+
+        def prep_weight_t(key, engs):
+            return prep(wts[key][:].bitcast(F32), "w", engs)
+
+        gw = prep_weight_t("t0", "sv")
+        grouped[(0, 0)] = prep(words_of(0, 0), "h", "sv")
+        wcodes["t0"] = quant(gw, const, "wt0")
+        gw = prep_weight_t("u0", "sv")
+        codes[(0, 0)] = quant(grouped[(0, 0)], cod, "h")
+        grouped[(0, 1)] = prep(words_of(0, 1), "a", "sv")
+        wcodes["u0"] = quant(gw, const, "wu0")
+        codes[(0, 1)] = quant(grouped[(0, 1)], cod, "a")
         nc.vector.tensor_copy(out=brow32[:], in_=brow[:])
         nc.vector.tensor_copy(out=step[:], in_=step_bf[:])
-        psb = bank()
+        psb = bank_pair()[0]
         nc.tensor.transpose(psb[:, 0:P], brow32[:], ident[:])
         nc.vector.tensor_copy(out=bias[:], in_=psb[:, 0:16])
         nc.scalar.mul(out=bhalf[:], in_=bias[:], mul=0.5)
-        group_in(1, "sv")
-        group_quantise(1)
+        for op in range(2):
+            grouped[(1, op)] = prep(words_of(1, op), "ha"[op], "sv")
+        load_weight("t1", Wt_out)
+        load_weight("u1", Wu_out)
 
-        to_quantise = []
-        products = {}
-        results = {}
+        extra = {3: "t1", 5: "u1"}
+        pending_w = []
 
-        for n in range(HALVES + 1):
-            i, hh = n // 2, n % 2
-            if n < HALVES:
-                typ = BLOCKS[i // 2][2]
-                if n % 4 == 0 and 3 <= (i + 4) // 2 < 8:
-                    block_tiles((i + 4) // 2)
-                    load_block((i + 4) // 2, 0, 0, 1)
-                    load_block((i + 4) // 2, 1, 0, 1)
-                hc, hs = codes[(i, 0)]
-                ac, asc = codes[(i, 1)]
-                wtc, wtsc = wcodes["t%d" % typ]
-                wuc, wus = wcodes["u%d" % typ]
-                for fb in (2 * hh, 2 * hh + 1):
-                    cols = slice(128 * fb, 128 * fb + 128)
-                    ps_u = bank()
-                    nc.tensor.matmul_mx(
-                        out=ps_u[:], lhsT=wuc[:, cols].bitcast(FP8X4), lhsT_scale=wus[:, cols],
-                        rhs=ac[:].bitcast(FP8X4), rhs_scale=asc[:], start=True, stop=True,
-                    )
-                    ps_t = bank()
-                    nc.tensor.matmul_mx(
-                        out=ps_t[:], lhsT=wtc[:, cols].bitcast(FP8X4), lhsT_scale=wtsc[:, cols],
-                        rhs=hc[:].bitcast(FP8X4), rhs_scale=hs[:], start=True, stop=True,
-                    )
-                    dt = mid.tile([P, 512], F32, name="dt", tag="dt")
-                    bt_col = 8 * typ + fb
-                    bu_col = 8 * typ + 4 + fb
-                    nc.scalar.activation(
-                        out=dt[:], in_=ps_t[:], func=ACT.Tanh, bias=bhalf[:, bt_col : bt_col + 1], scale=0.5
-                    )
-                    mt = mid.tile([P, 512], F32, name="mt", tag="mt", bufs=6)
-                    nc.vector.scalar_tensor_tensor(
-                        out=mt[:], in0=ps_u[:], scalar=bias[:, bu_col : bu_col + 1], in1=dt[:],
-                        op0=ALU.add, op1=ALU.mult,
-                    )
-                    products[(i, fb)] = mt
-
-                for where, key, g_t, pool, tag in to_quantise:
-                    where[key] = quantise(g_t, pool, tag)
-                to_quantise = []
-
-                g = i + AHEAD
-                if g < GROUPS:
-                    g_t = transpose_in(words_of(g, hh), "ha"[hh], "ss")
-                    to_quantise.append((codes, (g, hh), g_t, cod, "ha"[hh]))
-                if n in LATE_WEIGHTS:
-                    key = LATE_WEIGHTS[n]
-                    g_t = transpose_in(wts[key][:].bitcast(F32), "w", "sv")
-                    to_quantise.append((wcodes, key, g_t, const, "w" + key))
-
-            i, hh = max(n - 1, 0) // 2, max(n - 1, 0) % 2
-            b, n0 = BLOCKS[i // 2][0], BLOCKS[i // 2][1]
+        for i in range(NG):
+            s_i = i // 2
+            typ = SUPER[s_i][2]
             j0 = 4 * (i % 2)
-            if hh == 0 and n > 0:
-                results[i] = res.tile([P, 4, H], F32, name="o", tag="o")
-            o = results.get(i)
-            h3 = xs[i // 2][0][:].rearrange("p (j k) -> p j k", j=8)
-            ov = out[b, n0 : n0 + 1024, :].rearrange("(p j) f -> p j f", j=8)
-            for fb in (2 * hh, 2 * hh + 1) if n > 0 else ():
+            if i % 2 == 0 and 3 <= (i + 4) // 2 < 8:
+                issue(load_super((i + 4) // 2, 1))
+            if i + 1 < NG:
+                for op in range(2):
+                    codes[(i + 1, op)] = quant(grouped[(i + 1, op)], cod, "ha"[op])
+            for key, g_t in pending_w:
+                wcodes[key] = quant(g_t, const, "w" + key)
+            pending_w = []
+            hc, hs = codes[(i, 0)]
+            ac, asc = codes[(i, 1)]
+            tc_, ts_ = wcodes["t%d" % typ]
+            uc_, us_ = wcodes["u%d" % typ]
+            mts = []
+            for fb in range(4):
                 cols = slice(128 * fb, 128 * fb + 128)
-                mt = products[(i, fb)]
-                ps = bank()
-                for jl in range(4):
-                    nc.tensor.transpose(ps[:, 128 * jl : 128 * jl + 128], mt[:, 128 * jl : 128 * jl + 128], ident[:])
-                p3 = ps[:].rearrange("p (j f) -> p j f", j=4)
-                if fb == 0:
-                    ms = mid.tile([P, 4, P], F32, name="ms", tag="ms", bufs=2)
-                    nc.scalar.activation(out=ms[:], in_=p3, func=ACT.Copy, scale=step[:, 0:1])
-                    nc.gpsimd.tensor_tensor(out=o[:, :, cols], in0=ms[:], in1=h3[:, j0 : j0 + 4, cols], op=ALU.add)
-                else:
-                    nc.vector.scalar_tensor_tensor(
-                        out=o[:, :, cols], in0=p3, scalar=step[:, 0:1], in1=h3[:, j0 : j0 + 4, cols],
-                        op0=ALU.mult, op1=ALU.add,
-                    )
-            if n > 0 and i == GROUPS - 1:
-                pair = slice(256 * hh, 256 * hh + 256)
-                nc.sync.dma_start(out=ov[:, j0 : j0 + 4, pair], in_=o[:, :, pair])
-            elif n > 0 and hh == 1:
-                nc.sync.dma_start(out=ov[:, j0 : j0 + 4, :], in_=o[:])
+                ps_u, ps_t = bank_pair()
+                nc.tensor.matmul_mx(
+                    out=ps_u, lhsT=uc_[:, cols].bitcast(FP8X4), lhsT_scale=us_[:, cols],
+                    rhs=ac[:].bitcast(FP8X4), rhs_scale=asc[:], start=True, stop=True,
+                )
+                nc.tensor.matmul_mx(
+                    out=ps_t, lhsT=tc_[:, cols].bitcast(FP8X4), lhsT_scale=ts_[:, cols],
+                    rhs=hc[:].bitcast(FP8X4), rhs_scale=hs[:], start=True, stop=True,
+                )
+                dt = mid.tile([P, 512], F32, name="dt", tag="dt")
+                bt_col = 8 * typ + fb
+                bu_col = 8 * typ + 4 + fb
+                nc.scalar.activation(
+                    out=dt[:], in_=ps_t, func=ACT.Tanh, bias=bhalf[:, bt_col : bt_col + 1], scale=0.5
+                )
+                mt = mid.tile([P, 512], F32, name="mt", tag="mt", bufs=6)
+                nc.vector.scalar_tensor_tensor(
+                    out=mt[:], in0=ps_u, scalar=bias[:, bu_col : bu_col + 1], in1=dt[:], op0=ALU.add, op1=ALU.mult
+                )
+                mts.append(mt)
+
+            o = res.tile([P, 4, H], F32, name="o", tag="o")
+            h3 = xs[s_i][0][:].rearrange("p (j k) -> p j k", j=8)
+
+            def t_out(fbs):
+                pair = bank_pair()
+                for ps, fb in zip(pair, fbs):
+                    for jl in range(4):
+                        nc.tensor.transpose(
+                            ps[:, 128 * jl : 128 * jl + 128], mts[fb][:, 128 * jl : 128 * jl + 128], ident[:]
+                        )
+                for ps, fb in zip(pair, fbs):
+                    cols = slice(128 * fb, 128 * fb + 128)
+                    p3 = ps.rearrange("p (j f) -> p j f", j=4)
+                    if fb in GF:
+                        ms = mid.tile([P, 4, P], F32, name="ms", tag="ms", bufs=2)
+                        nc.scalar.activation(out=ms[:], in_=p3, func=ACT.Copy, scale=step[:, 0:1])
+                        nc.gpsimd.tensor_tensor(out=o[:, :, cols], in0=ms[:], in1=h3[:, j0 : j0 + 4, cols], op=ALU.add)
+                    else:
+                        nc.vector.scalar_tensor_tensor(
+                            out=o[:, :, cols], in0=p3, scalar=step[:, 0:1], in1=h3[:, j0 : j0 + 4, cols],
+                            op0=ALU.mult, op1=ALU.add,
+                        )
+
+            def t_next(op):
+                if i + 2 < NG:
+                    grouped[(i + 2, op)] = prep(words_of(i + 2, op), "ha"[op], "ss")
+
+            t_next(0)
+            t_out((0, 1))
+            t_next(1)
+            t_out((2, 3))
+            if i in extra:
+                pending_w.append((extra[i], prep_weight_t(extra[i], "sv")))
+            b, n0 = SUPER[s_i][0], SUPER[s_i][1]
+            ov = out[b, n0 : n0 + 1024, :].rearrange("(p j) f -> p j f", j=8)
+            nc.sync.dma_start(out=ov[:, j0 : j0 + 4, :], in_=o[:])

@@ -35,11 +35,10 @@ def tile_dynamicattentionnetwork_pb_t_kernel(
         cod = ctx.enter_context(tc.tile_pool(name="cod", bufs=2))
         mid = ctx.enter_context(tc.tile_pool(name="mid", bufs=3))
         res = ctx.enter_context(tc.tile_pool(name="res", bufs=3))
-        psum = ctx.enter_context(tc.psum_pool(name="psum", bufs=4))
+        psum = ctx.enter_context(tc.psum_pool(name="psum", bufs=8))
 
-        def bank_pair():
-            t = psum.tile([P, 1024], F32, name="pair", tag="pair")
-            return (t[:, 0:512], t[:, 512:1024])
+        def bank():
+            return psum.tile([P, 512], F32, name="bank", tag="bank")
 
         warm = const.tile([P, 1], F32, name="warm", tag="warm")
         nc.vector.memset(warm[:], 0.0)
@@ -84,16 +83,18 @@ def tile_dynamicattentionnetwork_pb_t_kernel(
             nc.sync.dma_start(out=t[:].rearrange("p (j k) -> p j k", j=4), in_=w.rearrange("(j p) k -> p j k", p=P))
             wts[key] = t
 
-        def t_in(ps, words, half):
-            pv = ps.rearrange("p (u r) -> p u r", u=2)
+        def t_in(words, half):
+            ps = bank()
+            pv = ps[:].rearrange("p (u r) -> p u r", u=2)
             for jj in range(2):
                 for u in range(2):
                     c0 = 256 * (2 * half + jj) + 128 * u
                     nc.tensor.transpose(pv[:, u, 128 * jj : 128 * jj + 128], words[:, c0 : c0 + 128], ident[:])
+            return ps
 
         def t_exit(eng, ps, g_tile, half):
             dst = g_tile[:].bitcast(F32)[:, 512 * half : 512 * half + 512].rearrange("p (r u) -> p r u", u=2)
-            src = ps.rearrange("p (u r) -> p r u", u=2)
+            src = ps[:].rearrange("p (u r) -> p r u", u=2)
             if eng == "s":
                 nc.scalar.copy(out=dst, in_=src)
             else:
@@ -123,34 +124,38 @@ def tile_dynamicattentionnetwork_pb_t_kernel(
         issue(load_super(1, 1))
         issue(load_super(2, 1))
 
-        def prep(words, tag, engs):
-            g_t = new_grouped(tag)
-            pair = bank_pair()
+        def prep_weight_t(key, engs):
+            g_t = new_grouped("w")
             for half in range(2):
-                t_in(pair[half], words, half)
-            for half in range(2):
-                t_exit(engs[half], pair[half], g_t, half)
+                ps = t_in(wts[key][:].bitcast(F32), half)
+                t_exit(engs[half], ps, g_t, half)
             return g_t
 
-        def prep_weight_t(key, engs):
-            return prep(wts[key][:].bitcast(F32), "w", engs)
-
         gw = prep_weight_t("t0", "sv")
-        grouped[(0, 0)] = prep(words_of(0, 0), "h", "sv")
+        grouped[(0, 0)] = new_grouped("h")
+        for half in range(2):
+            ps = t_in(words_of(0, 0), half)
+            t_exit("sv"[half], ps, grouped[(0, 0)], half)
         wcodes["t0"] = quant(gw, const, "wt0")
         gw = prep_weight_t("u0", "sv")
         codes[(0, 0)] = quant(grouped[(0, 0)], cod, "h")
-        grouped[(0, 1)] = prep(words_of(0, 1), "a", "sv")
+        grouped[(0, 1)] = new_grouped("a")
+        for half in range(2):
+            ps = t_in(words_of(0, 1), half)
+            t_exit("sv"[half], ps, grouped[(0, 1)], half)
         wcodes["u0"] = quant(gw, const, "wu0")
         codes[(0, 1)] = quant(grouped[(0, 1)], cod, "a")
         nc.vector.tensor_copy(out=brow32[:], in_=brow[:])
         nc.vector.tensor_copy(out=step[:], in_=step_bf[:])
-        psb = bank_pair()[0]
+        psb = bank()
         nc.tensor.transpose(psb[:, 0:P], brow32[:], ident[:])
         nc.vector.tensor_copy(out=bias[:], in_=psb[:, 0:16])
         nc.scalar.mul(out=bhalf[:], in_=bias[:], mul=0.5)
         for op in range(2):
-            grouped[(1, op)] = prep(words_of(1, op), "ha"[op], "sv")
+            grouped[(1, op)] = new_grouped("ha"[op])
+            for half in range(2):
+                ps = t_in(words_of(1, op), half)
+                t_exit("sv"[half], ps, grouped[(1, op)], half)
         load_weight("t1", Wt_out)
         load_weight("u1", Wu_out)
 
@@ -166,70 +171,93 @@ def tile_dynamicattentionnetwork_pb_t_kernel(
             if i + 1 < NG:
                 for op in range(2):
                     codes[(i + 1, op)] = quant(grouped[(i + 1, op)], cod, "ha"[op])
-            for key, g_t in pending_w:
-                wcodes[key] = quant(g_t, const, "w" + key)
-            pending_w = []
             hc, hs = codes[(i, 0)]
             ac, asc = codes[(i, 1)]
             tc_, ts_ = wcodes["t%d" % typ]
             uc_, us_ = wcodes["u%d" % typ]
             mts = []
-            for fb in range(4):
+            dts = []
+
+            def gate(fb):
                 cols = slice(128 * fb, 128 * fb + 128)
-                ps_u, ps_t = bank_pair()
+                ps_t = bank()
                 nc.tensor.matmul_mx(
-                    out=ps_u, lhsT=uc_[:, cols].bitcast(FP8X4), lhsT_scale=us_[:, cols],
-                    rhs=ac[:].bitcast(FP8X4), rhs_scale=asc[:], start=True, stop=True,
-                )
-                nc.tensor.matmul_mx(
-                    out=ps_t, lhsT=tc_[:, cols].bitcast(FP8X4), lhsT_scale=ts_[:, cols],
+                    out=ps_t[:], lhsT=tc_[:, cols].bitcast(FP8X4), lhsT_scale=ts_[:, cols],
                     rhs=hc[:].bitcast(FP8X4), rhs_scale=hs[:], start=True, stop=True,
                 )
-                dt = mid.tile([P, 512], F32, name="dt", tag="dt")
+                dt = mid.tile([P, 512], F32, name="dt", tag="dt", bufs=4)
                 bt_col = 8 * typ + fb
-                bu_col = 8 * typ + 4 + fb
                 nc.scalar.activation(
-                    out=dt[:], in_=ps_t, func=ACT.Tanh, bias=bhalf[:, bt_col : bt_col + 1], scale=0.5
+                    out=dt[:], in_=ps_t[:], func=ACT.Tanh, bias=bhalf[:, bt_col : bt_col + 1], scale=0.5
+                )
+                dts.append(dt)
+
+            def update(fb):
+                cols = slice(128 * fb, 128 * fb + 128)
+                ps_u = bank()
+                nc.tensor.matmul_mx(
+                    out=ps_u[:], lhsT=uc_[:, cols].bitcast(FP8X4), lhsT_scale=us_[:, cols],
+                    rhs=ac[:].bitcast(FP8X4), rhs_scale=asc[:], start=True, stop=True,
                 )
                 mt = mid.tile([P, 512], F32, name="mt", tag="mt", bufs=6)
+                bu_col = 8 * typ + 4 + fb
                 nc.vector.scalar_tensor_tensor(
-                    out=mt[:], in0=ps_u, scalar=bias[:, bu_col : bu_col + 1], in1=dt[:], op0=ALU.add, op1=ALU.mult
+                    out=mt[:], in0=ps_u[:], scalar=bias[:, bu_col : bu_col + 1], in1=dts[fb][:],
+                    op0=ALU.add, op1=ALU.mult,
                 )
                 mts.append(mt)
 
+            gate(0)
+            for fb in range(4):
+                if fb + 1 < 4:
+                    gate(fb + 1)
+                update(fb)
+
             o = res.tile([P, 4, H], F32, name="o", tag="o")
             h3 = xs[s_i][0][:].rearrange("p (j k) -> p j k", j=8)
-
-            def t_out(fbs):
-                pair = bank_pair()
-                for ps, fb in zip(pair, fbs):
-                    for jl in range(4):
-                        nc.tensor.transpose(
-                            ps[:, 128 * jl : 128 * jl + 128], mts[fb][:, 128 * jl : 128 * jl + 128], ident[:]
-                        )
-                for ps, fb in zip(pair, fbs):
-                    cols = slice(128 * fb, 128 * fb + 128)
-                    p3 = ps.rearrange("p (j f) -> p j f", j=4)
-                    if fb in GF:
-                        ms = mid.tile([P, 4, P], F32, name="ms", tag="ms", bufs=2)
-                        nc.scalar.activation(out=ms[:], in_=p3, func=ACT.Copy, scale=step[:, 0:1])
-                        nc.gpsimd.tensor_tensor(out=o[:, :, cols], in0=ms[:], in1=h3[:, j0 : j0 + 4, cols], op=ALU.add)
-                    else:
-                        nc.vector.scalar_tensor_tensor(
-                            out=o[:, :, cols], in0=p3, scalar=step[:, 0:1], in1=h3[:, j0 : j0 + 4, cols],
-                            op0=ALU.mult, op1=ALU.add,
-                        )
-
-            def t_next(op):
-                if i + 2 < NG:
-                    grouped[(i + 2, op)] = prep(words_of(i + 2, op), "ha"[op], "ss")
-
-            t_next(0)
-            t_out((0, 1))
-            t_next(1)
-            t_out((2, 3))
-            if i in extra:
-                pending_w.append((extra[i], prep_weight_t(extra[i], "sv")))
             b, n0 = SUPER[s_i][0], SUPER[s_i][1]
             ov = out[b, n0 : n0 + 1024, :].rearrange("(p j) f -> p j f", j=8)
-            nc.sync.dma_start(out=ov[:, j0 : j0 + 4, :], in_=o[:])
+
+            def t_out(fb):
+                ps = bank()
+                for jl in range(4):
+                    nc.tensor.transpose(ps[:, 128 * jl : 128 * jl + 128], mts[fb][:, 128 * jl : 128 * jl + 128], ident[:])
+                cols = slice(128 * fb, 128 * fb + 128)
+                p3 = ps[:].rearrange("p (j f) -> p j f", j=4)
+                if fb in GF:
+                    ms = mid.tile([P, 4, P], F32, name="ms", tag="ms", bufs=2)
+                    nc.scalar.activation(out=ms[:], in_=p3, func=ACT.Copy, scale=step[:, 0:1])
+                    nc.gpsimd.tensor_tensor(out=o[:, :, cols], in0=ms[:], in1=h3[:, j0 : j0 + 4, cols], op=ALU.add)
+                else:
+                    nc.vector.scalar_tensor_tensor(
+                        out=o[:, :, cols], in0=p3, scalar=step[:, 0:1], in1=h3[:, j0 : j0 + 4, cols],
+                        op0=ALU.mult, op1=ALU.add,
+                    )
+                if i == NG - 1:
+                    nc.sync.dma_start(out=ov[:, j0 : j0 + 4, cols], in_=o[:, :, cols])
+
+            def t_next(b):
+                g = i + 2
+                if g >= NG:
+                    return
+                op, half = b // 2, b % 2
+                if half == 0:
+                    grouped[(g, op)] = new_grouped("ha"[op])
+                ps = t_in(words_of(g, op), half)
+                t_exit("s", ps, grouped[(g, op)], half)
+
+            if i in extra:
+                pending_w.append((extra[i], prep_weight_t(extra[i], "ss")))
+            t_next(0)
+            t_next(1)
+            t_out(0)
+            t_next(2)
+            t_out(1)
+            t_next(3)
+            t_out(2)
+            t_out(3)
+            for key, g_t in pending_w:
+                wcodes[key] = quant(g_t, const, "w" + key)
+            pending_w = []
+            if i < NG - 1:
+                nc.sync.dma_start(out=ov[:, j0 : j0 + 4, :], in_=o[:])

@@ -19,7 +19,6 @@ FLOPS = 2 * 2 * 8192 * 512 * 512
 
 SUPER = [(0, 0, 0), (0, 1024, 0), (0, 2048, 0), (1, 0, 0), (1, 1024, 0), (1, 2048, 0), (0, 3072, 1), (1, 3072, 1)]
 NG = 16
-GF = (3,)
 
 
 def tile_dynamicattentionnetwork_pb_t_kernel(
@@ -43,45 +42,38 @@ def tile_dynamicattentionnetwork_pb_t_kernel(
         warm = const.tile([P, 1], F32, name="warm", tag="warm")
         nc.vector.memset(warm[:], 0.0)
         nc.scalar.activation(out=warm[:], in_=warm[:], func=ACT.Tanh)
-        ident = const.tile([P, P], F32, name="ident", tag="ident")
-        make_identity(nc, ident[:])
         brow = const.tile([P, P], BF16, name="brow", tag="brow")
         nc.vector.memset(brow[:], 0.0)
-        for n, b in enumerate((bt_inter, bu_inter, bt_out, bu_out)):
-            nc.scalar.dma_start(out=brow[4 * n : 4 * n + 4, :], in_=b.rearrange("(a c) -> a c", c=P))
+        ident = const.tile([P, P], F32, name="ident", tag="ident")
+        make_identity(nc, ident[:])
         step_bf = const.tile([P, 1], BF16, name="step_bf", tag="step_bf")
-        nc.scalar.dma_start(out=step_bf[:], in_=step_size.partition_broadcast(P))
         step = const.tile([P, 1], F32, name="step", tag="step")
         brow32 = const.tile([P, P], F32, name="brow32", tag="brow32")
         bias = const.tile([P, 16], F32, name="bias", tag="bias")
         bhalf = const.tile([P, 16], F32, name="bhalf", tag="bhalf")
 
         xs = {}
-
-        def load_super(s, parts):
-            b, n0 = SUPER[s][0], SUPER[s][1]
-            ht = xin.tile([P, 8 * H], BF16, name="h_sb", tag="h_sb")
-            at = xin.tile([P, 8 * H], BF16, name="a_sb", tag="a_sb")
-            xs[s] = (ht, at)
-            hv = hidden_states[b, n0 : n0 + 1024, :].rearrange("(p j) k -> p (j k)", j=8)
-            av = acc[b, n0 : n0 + 1024, :].rearrange("(p j) k -> p (j k)", j=8)
-            w = 8 * H // parts
-            todo = []
-            for c in range(parts):
-                todo.append((ht[:, c * w : (c + 1) * w], hv[:, c * w : (c + 1) * w]))
-                todo.append((at[:, c * w : (c + 1) * w], av[:, c * w : (c + 1) * w]))
-            return todo
-
-        def issue(todo):
-            for dst, src in todo:
-                nc.sync.dma_start(out=dst, in_=src)
-
         wts = {}
+        weights = {"t0": Wt_inter, "u0": Wu_inter, "t1": Wt_out, "u1": Wu_out}
 
-        def load_weight(key, w):
-            t = wraw.tile([P, 4 * H], BF16, name="w_sb", tag="w_sb")
-            nc.sync.dma_start(out=t[:].rearrange("p (j k) -> p j k", j=4), in_=w.rearrange("(j p) k -> p j k", p=P))
-            wts[key] = t
+        def load_rows(s, op, j0, j1):
+            b, n0 = SUPER[s][0], SUPER[s][1]
+            if (s, op) not in xs:
+                xs[(s, op)] = xin.tile([P, 8 * H], BF16, name="x_sb", tag="xa"[op] + "_sb")
+            src = (hidden_states, acc)[op][b, n0 : n0 + 1024, :].rearrange("(p j) k -> p (j k)", j=8)
+            nc.sync.dma_start(out=xs[(s, op)][:, j0 * H : j1 * H], in_=src[:, j0 * H : j1 * H])
+
+        def load_super(s):
+            load_rows(s, 0, 0, 8)
+            load_rows(s, 1, 0, 8)
+
+        def load_weight(key, halves):
+            if key not in wts:
+                wts[key] = wraw.tile([P, 4 * H], BF16, name="w_sb", tag="w_sb")
+            j0, j1 = 2 * halves[0], 2 * halves[-1] + 2
+            dst = wts[key][:].rearrange("p (j k) -> p j k", j=4)
+            src = weights[key].rearrange("(j p) k -> p j k", p=P)
+            nc.sync.dma_start(out=dst[:, j0:j1, :], in_=src[:, j0:j1, :])
 
         def t_in(words, half):
             ps = bank()
@@ -92,172 +84,192 @@ def tile_dynamicattentionnetwork_pb_t_kernel(
                     nc.tensor.transpose(pv[:, u, 128 * jj : 128 * jj + 128], words[:, c0 : c0 + 128], ident[:])
             return ps
 
-        def t_exit(eng, ps, g_tile, half):
-            dst = g_tile[:].bitcast(F32)[:, 512 * half : 512 * half + 512].rearrange("p (r u) -> p r u", u=2)
+        def t_exit(eng, ps, dst_bf):
+            dst = dst_bf.bitcast(F32).rearrange("p (r u) -> p r u", u=2)
             src = ps[:].rearrange("p (u r) -> p r u", u=2)
             if eng == "s":
                 nc.scalar.copy(out=dst, in_=src)
             else:
                 nc.vector.tensor_copy(out=dst, in_=src)
 
-        def quant(g_tile, pool, tag):
-            c = pool.tile([P, 512], U32, name="c_" + tag, tag="c_" + tag, align_bytes=64)
-            s = pool.tile([P, 512], U8, name="s_" + tag, tag="s_" + tag, align_bytes=64)
-            nc.vector.quantize_mx(out=c[:].bitcast(FP8X4), scales=s[:], in_=g_tile[:])
+        def quantize(codes, src, c0, n):
+            nc.vector.quantize_mx(
+                out=codes[0][:, c0 : c0 + n].bitcast(FP8X4), scales=codes[1][:, c0 : c0 + n],
+                in_=src[:, 4 * c0 : 4 * c0 + 4 * n],
+            )
+
+        def code_tiles(pool, tag, n):
+            c = pool.tile([P, n], U32, name="c_" + tag, tag="c_" + tag, align_bytes=64)
+            s = pool.tile([P, n], U8, name="s_" + tag, tag="s_" + tag, align_bytes=64)
             return (c, s)
-
-        def new_grouped(tag):
-            return grp.tile([P, 2048], BF16, name="g_" + tag, tag="g_" + tag, align_bytes=64)
-
-        def words_of(g, op):
-            return xs[g // 2][op][:].bitcast(F32)[:, 1024 * (g % 2) : 1024 * (g % 2) + 1024]
 
         grouped = {}
         codes = {}
         wcodes = {}
+        wgrouped = {}
+        dts = {}
+        mts = {}
+        outs = {}
 
-        first = load_super(0, 2)
-        load_weight("t0", Wt_inter)
-        issue(first[0:1])
-        load_weight("u0", Wu_inter)
-        issue(first[1:])
-        issue(load_super(1, 1))
-        issue(load_super(2, 1))
+        def prep_weight(key, half, eng):
+            if key not in wgrouped:
+                wgrouped[key] = grp.tile([P, 2048], BF16, name="g_w", tag="g_w", align_bytes=64)
+            t_exit(eng, t_in(wts[key][:].bitcast(F32), half), wgrouped[key][:, 1024 * half : 1024 * half + 1024])
 
-        def prep_weight_t(key, engs):
-            g_t = new_grouped("w")
+        def quant_weight(key, halves):
+            if key not in wcodes:
+                wcodes[key] = code_tiles(const, "w" + key, 512)
+            quantize(wcodes[key], wgrouped[key], 256 * halves[0], 256 * len(halves))
+
+        def prep_half(g, op, half, eng):
+            if g not in grouped:
+                grouped[g] = grp.tile([P, 4096], BF16, name="g_x", tag="g_x", align_bytes=64)
+            words = xs[(g // 2, op)][:].bitcast(F32)[:, 1024 * (g % 2) : 1024 * (g % 2) + 1024]
+            c0 = 2048 * op + 1024 * half
+            t_exit(eng, t_in(words, half), grouped[g][:, c0 : c0 + 1024])
+
+        def prep_input(g, op, engs):
             for half in range(2):
-                ps = t_in(wts[key][:].bitcast(F32), half)
-                t_exit(engs[half], ps, g_t, half)
-            return g_t
+                prep_half(g, op, half, engs[half])
 
-        gw = prep_weight_t("t0", "sv")
-        grouped[(0, 0)] = new_grouped("h")
-        for half in range(2):
-            ps = t_in(words_of(0, 0), half)
-            t_exit("sv"[half], ps, grouped[(0, 0)], half)
-        wcodes["t0"] = quant(gw, const, "wt0")
-        gw = prep_weight_t("u0", "sv")
-        codes[(0, 0)] = quant(grouped[(0, 0)], cod, "h")
-        grouped[(0, 1)] = new_grouped("a")
-        for half in range(2):
-            ps = t_in(words_of(0, 1), half)
-            t_exit("sv"[half], ps, grouped[(0, 1)], half)
-        wcodes["u0"] = quant(gw, const, "wu0")
-        codes[(0, 1)] = quant(grouped[(0, 1)], cod, "a")
-        nc.vector.tensor_copy(out=brow32[:], in_=brow[:])
-        nc.vector.tensor_copy(out=step[:], in_=step_bf[:])
+        def quant_input(g, ops):
+            if g not in codes:
+                codes[g] = code_tiles(cod, "x", 1024)
+            quantize(codes[g], grouped[g], 512 * ops[0], 512 * len(ops))
+
+        def product(key, g, op, fb):
+            ps = bank()
+            cols = slice(128 * fb, 128 * fb + 128)
+            rows = slice(512 * op, 512 * op + 512)
+            nc.tensor.matmul_mx(
+                out=ps[:], lhsT=wcodes[key][0][:, cols].bitcast(FP8X4), lhsT_scale=wcodes[key][1][:, cols],
+                rhs=codes[g][0][:, rows].bitcast(FP8X4), rhs_scale=codes[g][1][:, rows], start=True, stop=True,
+            )
+            return ps
+
+        def gate(i, fb):
+            typ = SUPER[i // 2][2]
+            ps = product("t%d" % typ, i, 0, fb)
+            dt = mid.tile([P, 512], F32, name="dt", tag="dt", bufs=4)
+            col = 8 * typ + fb
+            nc.scalar.activation(out=dt[:], in_=ps[:], func=ACT.Tanh, bias=bhalf[:, col : col + 1], scale=0.5)
+            dts[fb] = dt
+
+        def update(i, fb):
+            typ = SUPER[i // 2][2]
+            ps = product("u%d" % typ, i, 1, fb)
+            mt = mid.tile([P, 512], F32, name="mt", tag="mt", bufs=6)
+            col = 8 * typ + 4 + fb
+            nc.vector.scalar_tensor_tensor(
+                out=mt[:], in0=ps[:], scalar=bias[:, col : col + 1], in1=dts[fb][:], op0=ALU.add, op1=ALU.mult
+            )
+            mts[fb] = mt
+
+        def finish(i, o_part, p3, h_part, by_gpsimd):
+            if by_gpsimd:
+                ms = mid.tile([P, 4, P], F32, name="ms", tag="ms", bufs=2)
+                nc.scalar.activation(out=ms[:], in_=p3, func=ACT.Copy, scale=step[:, 0:1])
+                nc.gpsimd.tensor_tensor(out=o_part, in0=ms[:], in1=h_part, op=ALU.add)
+            else:
+                nc.vector.scalar_tensor_tensor(
+                    out=o_part, in0=p3, scalar=step[:, 0:1], in1=h_part, op0=ALU.mult, op1=ALU.add
+                )
+
+        def t_out(i, fb, by_gpsimd=False):
+            if fb == 0:
+                outs[i] = res.tile([P, 4, H], F32, name="o", tag="o")
+            j0 = 4 * (i % 2)
+            h3 = xs[(i // 2, 0)][:].rearrange("p (j k) -> p j k", j=8)
+            ps = bank()
+            for jl in range(4):
+                nc.tensor.transpose(ps[:, 128 * jl : 128 * jl + 128], mts[fb][:, 128 * jl : 128 * jl + 128], ident[:])
+            cols = slice(128 * fb, 128 * fb + 128)
+            p3 = ps[:].rearrange("p (j f) -> p j f", j=4)
+            finish(i, outs[i][:, :, cols], p3, h3[:, j0 : j0 + 4, cols], by_gpsimd)
+
+        def store(i, cols):
+            b, n0 = SUPER[i // 2][0], SUPER[i // 2][1]
+            j0 = 4 * (i % 2)
+            ov = out[b, n0 : n0 + 1024, :].rearrange("(p j) f -> p j f", j=8)
+            nc.sync.dma_start(out=ov[:, j0 : j0 + 4, cols], in_=outs[i][:, :, cols])
+
+        load_weight("t0", (0, 1))
+        load_rows(0, 0, 0, 4)
+        for n, b in enumerate((bt_inter, bu_inter, bt_out, bu_out)):
+            nc.sync.dma_start(out=brow[4 * n : 4 * n + 4, :], in_=b.rearrange("(a c) -> a c", c=P))
+        load_weight("u0", (0, 1))
+        load_rows(0, 1, 0, 4)
+        load_rows(0, 0, 4, 8)
+        load_rows(0, 1, 4, 8)
+        nc.sync.dma_start(out=step_bf[:], in_=step_size.partition_broadcast(P))
+        load_super(1)
+        load_super(2)
+
+        prep_weight("t0", 0, "s")
+        prep_weight("t0", 1, "s")
+        prep_input(0, 0, "vs")
+        quant_weight("t0", (0, 1))
+        quant_input(0, (0,))
+        nc.scalar.copy(out=brow32[:], in_=brow[:])
+        prep_weight("u0", 0, "s")
+        prep_weight("u0", 1, "v")
         psb = bank()
         nc.tensor.transpose(psb[:, 0:P], brow32[:], ident[:])
-        nc.vector.tensor_copy(out=bias[:], in_=psb[:, 0:16])
+        nc.scalar.copy(out=bias[:], in_=psb[:, 0:16])
         nc.scalar.mul(out=bhalf[:], in_=bias[:], mul=0.5)
-        for op in range(2):
-            grouped[(1, op)] = new_grouped("ha"[op])
-            for half in range(2):
-                ps = t_in(words_of(1, op), half)
-                t_exit("sv"[half], ps, grouped[(1, op)], half)
-        load_weight("t1", Wt_out)
-        load_weight("u1", Wu_out)
+        prep_input(0, 1, "vs")
+        gate(0, 0)
+        gate(0, 1)
+        quant_weight("u0", (0, 1))
+        quant_input(0, (1,))
+        gate(0, 2)
+        gate(0, 3)
+        prep_input(1, 0, "vs")
+        update(0, 0)
+        update(0, 1)
+        update(0, 2)
+        update(0, 3)
+        nc.vector.tensor_copy(out=step[:], in_=step_bf[:])
+        load_weight("t1", (0, 1))
+        load_weight("u1", (0, 1))
 
-        extra = {3: "t1", 5: "u1"}
-        pending_w = []
+        late = {3: "t1", 5: "u1"}
 
         for i in range(NG):
-            s_i = i // 2
-            typ = SUPER[s_i][2]
-            j0 = 4 * (i % 2)
-            if i % 2 == 0 and 3 <= (i + 4) // 2 < 8:
-                issue(load_super((i + 4) // 2, 1))
-            if i + 1 < NG:
-                for op in range(2):
-                    codes[(i + 1, op)] = quant(grouped[(i + 1, op)], cod, "ha"[op])
-            hc, hs = codes[(i, 0)]
-            ac, asc = codes[(i, 1)]
-            tc_, ts_ = wcodes["t%d" % typ]
-            uc_, us_ = wcodes["u%d" % typ]
-            mts = []
-            dts = []
-
-            def gate(fb):
-                cols = slice(128 * fb, 128 * fb + 128)
-                ps_t = bank()
-                nc.tensor.matmul_mx(
-                    out=ps_t[:], lhsT=tc_[:, cols].bitcast(FP8X4), lhsT_scale=ts_[:, cols],
-                    rhs=hc[:].bitcast(FP8X4), rhs_scale=hs[:], start=True, stop=True,
-                )
-                dt = mid.tile([P, 512], F32, name="dt", tag="dt", bufs=4)
-                bt_col = 8 * typ + fb
-                nc.scalar.activation(
-                    out=dt[:], in_=ps_t[:], func=ACT.Tanh, bias=bhalf[:, bt_col : bt_col + 1], scale=0.5
-                )
-                dts.append(dt)
-
-            def update(fb):
-                cols = slice(128 * fb, 128 * fb + 128)
-                ps_u = bank()
-                nc.tensor.matmul_mx(
-                    out=ps_u[:], lhsT=uc_[:, cols].bitcast(FP8X4), lhsT_scale=us_[:, cols],
-                    rhs=ac[:].bitcast(FP8X4), rhs_scale=asc[:], start=True, stop=True,
-                )
-                mt = mid.tile([P, 512], F32, name="mt", tag="mt", bufs=6)
-                bu_col = 8 * typ + 4 + fb
-                nc.vector.scalar_tensor_tensor(
-                    out=mt[:], in0=ps_u[:], scalar=bias[:, bu_col : bu_col + 1], in1=dts[fb][:],
-                    op0=ALU.add, op1=ALU.mult,
-                )
-                mts.append(mt)
-
-            gate(0)
-            for fb in range(4):
-                if fb + 1 < 4:
-                    gate(fb + 1)
-                update(fb)
-
-            o = res.tile([P, 4, H], F32, name="o", tag="o")
-            h3 = xs[s_i][0][:].rearrange("p (j k) -> p j k", j=8)
-            b, n0 = SUPER[s_i][0], SUPER[s_i][1]
-            ov = out[b, n0 : n0 + 1024, :].rearrange("(p j) f -> p j f", j=8)
-
-            def t_out(fb):
-                ps = bank()
-                for jl in range(4):
-                    nc.tensor.transpose(ps[:, 128 * jl : 128 * jl + 128], mts[fb][:, 128 * jl : 128 * jl + 128], ident[:])
-                cols = slice(128 * fb, 128 * fb + 128)
-                p3 = ps[:].rearrange("p (j f) -> p j f", j=4)
-                if fb in GF:
-                    ms = mid.tile([P, 4, P], F32, name="ms", tag="ms", bufs=2)
-                    nc.scalar.activation(out=ms[:], in_=p3, func=ACT.Copy, scale=step[:, 0:1])
-                    nc.gpsimd.tensor_tensor(out=o[:, :, cols], in0=ms[:], in1=h3[:, j0 : j0 + 4, cols], op=ALU.add)
-                else:
-                    nc.vector.scalar_tensor_tensor(
-                        out=o[:, :, cols], in0=p3, scalar=step[:, 0:1], in1=h3[:, j0 : j0 + 4, cols],
-                        op0=ALU.mult, op1=ALU.add,
-                    )
-                if i == NG - 1:
-                    nc.sync.dma_start(out=ov[:, j0 : j0 + 4, cols], in_=o[:, :, cols])
-
-            def t_next(b):
-                g = i + 2
-                if g >= NG:
-                    return
-                op, half = b // 2, b % 2
-                if half == 0:
-                    grouped[(g, op)] = new_grouped("ha"[op])
-                ps = t_in(words_of(g, op), half)
-                t_exit("s", ps, grouped[(g, op)], half)
-
-            if i in extra:
-                pending_w.append((extra[i], prep_weight_t(extra[i], "ss")))
-            t_next(0)
-            t_next(1)
-            t_out(0)
-            t_next(2)
-            t_out(1)
-            t_next(3)
-            t_out(2)
-            t_out(3)
-            for key, g_t in pending_w:
-                wcodes[key] = quant(g_t, const, "w" + key)
-            pending_w = []
-            if i < NG - 1:
-                nc.sync.dma_start(out=ov[:, j0 : j0 + 4, :], in_=o[:])
+            if i % 2 == 0 and 3 <= i // 2 + 2 < 8:
+                load_super(i // 2 + 2)
+            if i > 0:
+                if i + 1 < NG:
+                    quant_input(i + 1, (0, 1))
+                gate(i, 0)
+                for fb in range(4):
+                    if fb + 1 < 4:
+                        gate(i, fb + 1)
+                    update(i, fb)
+            else:
+                prep_input(1, 1, "ss")
+                quant_input(1, (0, 1))
+            if i in late:
+                for half in range(2):
+                    prep_weight(late[i], half, "s")
+            gf = () if i == NG - 1 else (3,)
+            for half in range(2):
+                if i + 2 < NG:
+                    prep_half(i + 2, 0, half, "s")
+            t_out(i, 0, 0 in gf)
+            if i == NG - 1:
+                store(i, slice(0, 128))
+            if i + 2 < NG:
+                prep_half(i + 2, 1, 0, "s")
+            t_out(i, 1, 1 in gf)
+            if i == NG - 1:
+                store(i, slice(128, 256))
+            if i + 2 < NG:
+                prep_half(i + 2, 1, 1, "s")
+            t_out(i, 2, 2 in gf)
+            if i == NG - 1:
+                store(i, slice(256, 384))
+            t_out(i, 3, 3 in gf)
+            if i in late:
+                quant_weight(late[i], (0, 1))
+            store(i, slice(384, H) if i == NG - 1 else slice(0, H))

@@ -233,7 +233,7 @@ def tile_dynamicattentionnetwork_pb_t_kernel(
         load_weight("t1", (0, 1))
         load_weight("u1", (0, 1))
 
-        late = {3: "t1", 5: "u1"}
+        late = {2: ("t1", 0), 4: ("t1", 1), 6: ("u1", 0), 8: ("u1", 1)}
 
         for i in range(NG):
             if i % 2 == 0 and 3 <= i // 2 + 2 < 8:
@@ -242,16 +242,19 @@ def tile_dynamicattentionnetwork_pb_t_kernel(
                 if i + 1 < NG:
                     quant_input(i + 1, (0, 1))
                 gate(i, 0)
-                for fb in range(4):
-                    if fb + 1 < 4:
-                        gate(i, fb + 1)
-                    update(i, fb)
+                gate(i, 1)
+                gate(i, 2)
+                update(i, 0)
+                gate(i, 3)
+                update(i, 1)
+                update(i, 2)
+                update(i, 3)
             else:
                 prep_input(1, 1, "ss")
-                quant_input(1, (0, 1))
+                quant_input(1, (0,))
+                quant_input(1, (1,))
             if i in late:
-                for half in range(2):
-                    prep_weight(late[i], half, "s")
+                prep_weight(*late[i], "s")
             gf = () if i == NG - 1 else (3,)
             for half in range(2):
                 if i + 2 < NG:
@@ -271,5 +274,6 @@ def tile_dynamicattentionnetwork_pb_t_kernel(
                 store(i, slice(256, 384))
             t_out(i, 3, 3 in gf)
             if i in late:
-                quant_weight(late[i], (0, 1))
+                key, half = late[i]
+                quant_weight(key, (half,))
             store(i, slice(384, H) if i == NG - 1 else slice(0, H))

@@ -169,11 +169,21 @@ def tile_dynamicattentionnetwork_pb_t_kernel(
             if by_gpsimd:
                 ms = mid.tile([P, 4, P], F32, name="ms", tag="ms", bufs=2)
                 nc.scalar.activation(out=ms[:], in_=p3, func=ACT.Copy, scale=step[:, 0:1])
-                nc.gpsimd.tensor_tensor(out=o_part, in0=ms[:], in1=h_part, op=ALU.add)
+                waiting.append((i, o_part, ms, h_part))
             else:
                 nc.vector.scalar_tensor_tensor(
                     out=o_part, in0=p3, scalar=step[:, 0:1], in1=h_part, op0=ALU.mult, op1=ALU.add
                 )
+
+        waiting = []
+        mark = const.tile([P, 1], U32, name="mark", tag="mark")
+
+        def add_on_gpsimd(quantised):
+            i, o_part, ms, h_part = waiting.pop()
+            if quantised < NG:
+                nc.gpsimd.tensor_copy(out=mark[:], in_=codes[quantised][0][:, 0:1])
+            nc.gpsimd.tensor_tensor(out=o_part, in0=ms[:], in1=h_part, op=ALU.add)
+            store(i, slice(0, H))
 
         def t_out(i, fb, by_gpsimd=False):
             if fb == 0:
@@ -202,7 +212,9 @@ def tile_dynamicattentionnetwork_pb_t_kernel(
         load_rows(0, 0, 4, 8)
         load_rows(0, 1, 4, 8)
         nc.sync.dma_start(out=step_bf[:], in_=step_size.partition_broadcast(P))
-        load_super(1)
+        for j0 in (0, 4):
+            for op in range(2):
+                load_rows(1, op, j0, j0 + 4)
         load_super(2)
 
         prep_weight("t0", 0, "s")
@@ -236,17 +248,18 @@ def tile_dynamicattentionnetwork_pb_t_kernel(
         late = {2: ("t1", 0), 4: ("t1", 1), 6: ("u1", 0), 8: ("u1", 1)}
 
         for i in range(NG):
-            if i % 2 == 0 and 3 <= i // 2 + 2 < 8:
-                load_super(i // 2 + 2)
             if i > 0:
                 if i + 1 < NG:
                     quant_input(i + 1, (0, 1))
+                add_on_gpsimd(i + 1)
+                if i % 2 == 0 and i // 2 + 2 < 8:
+                    load_super(i // 2 + 2)
                 gate(i, 0)
                 gate(i, 1)
-                gate(i, 2)
                 update(i, 0)
-                gate(i, 3)
+                gate(i, 2)
                 update(i, 1)
+                gate(i, 3)
                 update(i, 2)
                 update(i, 3)
             else:
@@ -276,4 +289,5 @@ def tile_dynamicattentionnetwork_pb_t_kernel(
             if i in late:
                 key, half = late[i]
                 quant_weight(key, (half,))
-            store(i, slice(384, H) if i == NG - 1 else slice(0, H))
+            if i == NG - 1:
+                store(i, slice(384, H))

from contextlib import ExitStack

import concourse.bass as bass
import concourse.mybir as mybir
import concourse.tile as tile
from concourse.masks import make_identity

F32 = mybir.dt.float32
BF16 = mybir.dt.bfloat16
U32 = mybir.dt.uint32
U8 = mybir.dt.uint8
FP8X4 = mybir.dt.float8_e4m3fn_x4
ACT = mybir.ActivationFunctionType
ALU = mybir.AluOpType

P = 128
H = 512
FLOPS = 2 * 2 * 8192 * 512 * 512

SUPER = [(0, 0, 0), (0, 1024, 0), (0, 2048, 0), (1, 0, 0), (1, 1024, 0), (1, 2048, 0), (0, 3072, 1), (1, 3072, 1)]
NG = 16


def tile_dynamicattentionnetwork_pb_t_kernel(
    tc, hidden_states, acc, Wu_inter, bu_inter, Wt_inter, bt_inter, Wu_out, bu_out, Wt_out, bt_out, step_size, out
):
    nc = tc.nc
    with ExitStack() as ctx:
        ctx.enter_context(tc.manual_schedule())
        const = ctx.enter_context(tc.tile_pool(name="const", bufs=1))
        xin = ctx.enter_context(tc.tile_pool(name="xin", bufs=3))
        wraw = ctx.enter_context(tc.tile_pool(name="wraw", bufs=2))
        grp = ctx.enter_context(tc.tile_pool(name="grp", bufs=2))
        cod = ctx.enter_context(tc.tile_pool(name="cod", bufs=2))
        mid = ctx.enter_context(tc.tile_pool(name="mid", bufs=3))
        res = ctx.enter_context(tc.tile_pool(name="res", bufs=3))
        psum = ctx.enter_context(tc.psum_pool(name="psum", bufs=8))

        def bank():
            return psum.tile([P, 512], F32, name="bank", tag="bank")

        warm = const.tile([P, 1], F32, name="warm", tag="warm")
        nc.vector.memset(warm[:], 0.0)
        nc.scalar.activation(out=warm[:], in_=warm[:], func=ACT.Tanh)
        brow = const.tile([P, P], BF16, name="brow", tag="brow")
        nc.vector.memset(brow[:], 0.0)
        ident = const.tile([P, P], F32, name="ident", tag="ident")
        make_identity(nc, ident[:])
        step_bf = const.tile([P, 1], BF16, name="step_bf", tag="step_bf")
        step = const.tile([P, 1], F32, name="step", tag="step")
        brow32 = const.tile([P, P], F32, name="brow32", tag="brow32")
        bias = const.tile([P, 16], F32, name="bias", tag="bias")
        bhalf = const.tile([P, 16], F32, name="bhalf", tag="bhalf")

        xs = {}
        wts = {}
        weights = {"t0": Wt_inter, "u0": Wu_inter, "t1": Wt_out, "u1": Wu_out}

        def load_rows(s, op, j0, j1):
            b, n0 = SUPER[s][0], SUPER[s][1]
            if (s, op) not in xs:
                xs[(s, op)] = xin.tile([P, 8 * H], BF16, name="x_sb", tag="xa"[op] + "_sb")
            src = (hidden_states, acc)[op][b, n0 : n0 + 1024, :].rearrange("(p j) k -> p (j k)", j=8)
            nc.sync.dma_start(out=xs[(s, op)][:, j0 * H : j1 * H], in_=src[:, j0 * H : j1 * H])

        def load_super(s):
            load_rows(s, 0, 0, 8)
            load_rows(s, 1, 0, 8)

        def load_weight(key, halves):
            if key not in wts:
                wts[key] = wraw.tile([P, 4 * H], BF16, name="w_sb", tag="w_sb")
            j0, j1 = 2 * halves[0], 2 * halves[-1] + 2
            dst = wts[key][:].rearrange("p (j k) -> p j k", j=4)
            src = weights[key].rearrange("(j p) k -> p j k", p=P)
            nc.sync.dma_start(out=dst[:, j0:j1, :], in_=src[:, j0:j1, :])

        def t_in(words, half):
            ps = bank()
            pv = ps[:].rearrange("p (u r) -> p u r", u=2)
            for jj in range(2):
                for u in range(2):
                    c0 = 256 * (2 * half + jj) + 128 * u
                    nc.tensor.transpose(pv[:, u, 128 * jj : 128 * jj + 128], words[:, c0 : c0 + 128], ident[:])
            return ps

        def t_exit(eng, ps, dst_bf):
            dst = dst_bf.bitcast(F32).rearrange("p (r u) -> p r u", u=2)
            src = ps[:].rearrange("p (u r) -> p r u", u=2)
            if eng == "s":
                nc.scalar.copy(out=dst, in_=src)
            else:
                nc.vector.tensor_copy(out=dst, in_=src)

        def quantize(codes, src, c0, n):
            nc.vector.quantize_mx(
                out=codes[0][:, c0 : c0 + n].bitcast(FP8X4), scales=codes[1][:, c0 : c0 + n],
                in_=src[:, 4 * c0 : 4 * c0 + 4 * n],
            )

        def code_tiles(pool, tag, n):
            c = pool.tile([P, n], U32, name="c_" + tag, tag="c_" + tag, align_bytes=64)
            s = pool.tile([P, n], U8, name="s_" + tag, tag="s_" + tag, align_bytes=64)
            return (c, s)

        grouped = {}
        codes = {}
        wcodes = {}
        wgrouped = {}
        dts = {}
        mts = {}
        outs = {}

        def prep_weight(key, half, eng):
            if key not in wgrouped:
                wgrouped[key] = grp.tile([P, 2048], BF16, name="g_w", tag="g_w", align_bytes=64)
            t_exit(eng, t_in(wts[key][:].bitcast(F32), half), wgrouped[key][:, 1024 * half : 1024 * half + 1024])

        def quant_weight(key, halves):
            if key not in wcodes:
                wcodes[key] = code_tiles(const, "w" + key, 512)
            quantize(wcodes[key], wgrouped[key], 256 * halves[0], 256 * len(halves))

        def prep_half(g, op, half, eng):
            if g not in grouped:
                grouped[g] = grp.tile([P, 4096], BF16, name="g_x", tag="g_x", align_bytes=64)
            words = xs[(g // 2, op)][:].bitcast(F32)[:, 1024 * (g % 2) : 1024 * (g % 2) + 1024]
            c0 = 2048 * op + 1024 * half
            t_exit(eng, t_in(words, half), grouped[g][:, c0 : c0 + 1024])

        def prep_input(g, op, engs):
            for half in range(2):
                prep_half(g, op, half, engs[half])

        def quant_input(g, ops):
            if g not in codes:
                codes[g] = code_tiles(cod, "x", 1024)
            quantize(codes[g], grouped[g], 512 * ops[0], 512 * len(ops))

        def product(key, g, op, fb):
            ps = bank()
            cols = slice(128 * fb, 128 * fb + 128)
            rows = slice(512 * op, 512 * op + 512)
            nc.tensor.matmul_mx(
                out=ps[:], lhsT=wcodes[key][0][:, cols].bitcast(FP8X4), lhsT_scale=wcodes[key][1][:, cols],
                rhs=codes[g][0][:, rows].bitcast(FP8X4), rhs_scale=codes[g][1][:, rows], start=True, stop=True,
            )
            return ps

        def gate(i, fb):
            typ = SUPER[i // 2][2]
            ps = product("t%d" % typ, i, 0, fb)
            dt = mid.tile([P, 512], F32, name="dt", tag="dt", bufs=4)
            col = 8 * typ + fb
            nc.scalar.activation(out=dt[:], in_=ps[:], func=ACT.Tanh, bias=bhalf[:, col : col + 1], scale=0.5)
            dts[fb] = dt

        def update(i, fb):
            typ = SUPER[i // 2][2]
            ps = product("u%d" % typ, i, 1, fb)
            mt = mid.tile([P, 512], F32, name="mt", tag="mt", bufs=6)
            col = 8 * typ + 4 + fb
            nc.vector.scalar_tensor_tensor(
                out=mt[:], in0=ps[:], scalar=bias[:, col : col + 1], in1=dts[fb][:], op0=ALU.add, op1=ALU.mult
            )
            mts[fb] = mt

        def finish(i, o_part, p3, h_part, by_gpsimd):
            if by_gpsimd:
                ms = mid.tile([P, 4, P], F32, name="ms", tag="ms", bufs=2)
                nc.scalar.activation(out=ms[:], in_=p3, func=ACT.Copy, scale=step[:, 0:1])
                waiting.append((i, o_part, ms, h_part))
            else:
                nc.vector.scalar_tensor_tensor(
                    out=o_part, in0=p3, scalar=step[:, 0:1], in1=h_part, op0=ALU.mult, op1=ALU.add
                )

        waiting = []
        mark = const.tile([P, 1], U32, name="mark", tag="mark")

        def add_on_gpsimd(quantised):
            i, o_part, ms, h_part = waiting.pop()
            if quantised < NG:
                nc.gpsimd.tensor_copy(out=mark[:], in_=codes[quantised][0][:, 0:1])
            nc.gpsimd.tensor_tensor(out=o_part, in0=ms[:], in1=h_part, op=ALU.add)
            store(i, slice(0, H))

        def t_out(i, fb, by_gpsimd=False):
            if fb == 0:
                outs[i] = res.tile([P, 4, H], F32, name="o", tag="o")
            j0 = 4 * (i % 2)
            h3 = xs[(i // 2, 0)][:].rearrange("p (j k) -> p j k", j=8)
            ps = bank()
            for jl in range(4):
                nc.tensor.transpose(ps[:, 128 * jl : 128 * jl + 128], mts[fb][:, 128 * jl : 128 * jl + 128], ident[:])
            cols = slice(128 * fb, 128 * fb + 128)
            p3 = ps[:].rearrange("p (j f) -> p j f", j=4)
            finish(i, outs[i][:, :, cols], p3, h3[:, j0 : j0 + 4, cols], by_gpsimd)

        def store(i, cols):
            b, n0 = SUPER[i // 2][0], SUPER[i // 2][1]
            j0 = 4 * (i % 2)
            ov = out[b, n0 : n0 + 1024, :].rearrange("(p j) f -> p j f", j=8)
            nc.sync.dma_start(out=ov[:, j0 : j0 + 4, cols], in_=outs[i][:, :, cols])

        load_weight("t0", (0, 1))
        load_rows(0, 0, 0, 4)
        for n, b in enumerate((bt_inter, bu_inter, bt_out, bu_out)):
            nc.sync.dma_start(out=brow[4 * n : 4 * n + 4, :], in_=b.rearrange("(a c) -> a c", c=P))
        load_weight("u0", (0, 1))
        load_rows(0, 1, 0, 4)
        load_rows(0, 0, 4, 8)
        load_rows(0, 1, 4, 8)
        nc.sync.dma_start(out=step_bf[:], in_=step_size.partition_broadcast(P))
        for j0 in (0, 4):
            for op in range(2):
                load_rows(1, op, j0, j0 + 4)
        load_super(2)

        prep_weight("t0", 0, "s")
        prep_weight("t0", 1, "s")
        prep_input(0, 0, "vs")
        quant_weight("t0", (0, 1))
        quant_input(0, (0,))
        nc.scalar.copy(out=brow32[:], in_=brow[:])
        prep_weight("u0", 0, "s")
        prep_weight("u0", 1, "v")
        psb = bank()
        nc.tensor.transpose(psb[:, 0:P], brow32[:], ident[:])
        nc.scalar.copy(out=bias[:], in_=psb[:, 0:16])
        nc.scalar.mul(out=bhalf[:], in_=bias[:], mul=0.5)
        prep_input(0, 1, "vs")
        gate(0, 0)
        gate(0, 1)
        quant_weight("u0", (0, 1))
        quant_input(0, (1,))
        gate(0, 2)
        gate(0, 3)
        prep_input(1, 0, "vs")
        update(0, 0)
        update(0, 1)
        update(0, 2)
        update(0, 3)
        nc.vector.tensor_copy(out=step[:], in_=step_bf[:])
        load_weight("t1", (0, 1))
        load_weight("u1", (0, 1))

        late = {2: ("t1", 0), 4: ("t1", 1), 6: ("u1", 0), 8: ("u1", 1)}

        for i in range(NG):
            if i > 0:
                if i + 1 < NG:
                    quant_input(i + 1, (0, 1))
                add_on_gpsimd(i + 1)
                if i % 2 == 0 and i // 2 + 2 < 8:
                    load_super(i // 2 + 2)
                gate(i, 0)
                gate(i, 1)
                update(i, 0)
                gate(i, 2)
                update(i, 1)
                gate(i, 3)
                update(i, 2)
                update(i, 3)
            else:
                prep_input(1, 1, "ss")
                quant_input(1, (0,))
                quant_input(1, (1,))
            if i in late:
                prep_weight(*late[i], "s")
            gf = () if i == NG - 1 else (3,)
            for half in range(2):
                if i + 2 < NG:
                    prep_half(i + 2, 0, half, "s")
            t_out(i, 0, 0 in gf)
            if i == NG - 1:
                store(i, slice(0, 128))
            if i + 2 < NG:
                prep_half(i + 2, 1, 0, "s")
            t_out(i, 1, 1 in gf)
            if i == NG - 1:
                store(i, slice(128, 256))
            if i + 2 < NG:
                prep_half(i + 2, 1, 1, "s")
            t_out(i, 2, 2 in gf)
            if i == NG - 1:
                store(i, slice(256, 384))
            t_out(i, 3, 3 in gf)
            if i in late:
                key, half = late[i]
                quant_weight(key, (half,))
            if i == NG - 1:
                store(i, slice(384, H))
